import numpy as np
import ml_dtypes


def mxq(x, axis, fmt="e4m3"):
    dtype, down = {"e4m3": (ml_dtypes.float8_e4m3fn, 7), "e5m2": (ml_dtypes.float8_e5m2, 14)}[fmt]
    v = np.moveaxis(np.asarray(x, np.float32).astype(ml_dtypes.bfloat16).astype(np.float64), axis, -1)
    blocks = v.reshape(v.shape[:-1] + (-1, 32))
    amax = np.abs(blocks).max(-1, keepdims=True)
    byte = np.maximum(np.where(amax > 0, np.frexp(amax)[1] - 1 + 127, 0) - down, 1)
    scale = np.exp2(byte - 127.0)
    codes = (blocks / scale).astype(np.float32).astype(dtype).astype(np.float64)
    return np.moveaxis((codes * scale).reshape(v.shape), -1, axis)


WIDE = False


def mx_kscale(k):
    if not WIDE:
        return np.ones(k)
    levels = np.array([10, -10, 5, -5, 0])
    a = np.random.permutation(np.resize(levels, k // 512 * 4)).reshape(k // 512, 4)
    idx = np.arange(k)
    return np.exp2(a[idx // 512, idx % 128 // 32])


BF16 = ml_dtypes.bfloat16


def bf(x):
    return np.asarray(x, np.float32).astype(BF16)


def f64(x):
    return np.asarray(x).astype(np.float64)


B, N, NODE_IN, EDGE_IN, EDGE_OUT = 2, 32, 384, 256, 1024
D_IN = 2 * NODE_IN + EDGE_IN
HID = 2 * EDGE_OUT
NEG_SLOPE = 0.1


def leaky_relu(v):
    return np.where(v >= 0.0, v, NEG_SLOPE * v)


def setup_inputs():
    s = mx_kscale(D_IN)
    sn, se = s[:NODE_IN], s[2 * NODE_IN:]
    st = np.concatenate([sn, sn, se])
    return {"node_fts": bf(np.random.standard_normal((B, N, NODE_IN)) * sn),
            "edge_fts": bf(np.random.standard_normal((B, N * N, EDGE_IN)) * se),
            "Wt": bf(np.random.standard_normal((HID, D_IN)) / np.sqrt(D_IN) / st)}


def reference(node_fts, edge_fts, Wt):
    node = f64(node_fts)
    src = np.repeat(node, N, axis=1)
    dst = np.tile(node, (1, N, 1))
    triplet = np.concatenate([src, dst, f64(edge_fts)], axis=-1)
    return leaky_relu(mxq(triplet, 2, "e4m3") @ mxq(f64(Wt).T, 0, "e4m3"))

@@ -1,0 +1,185 @@
+from contextlib import ExitStack
+
+import concourse.mybir as mybir
+from concourse.masks import make_identity
+
+F32 = mybir.dt.float32
+BF16 = mybir.dt.bfloat16
+I32 = mybir.dt.int32
+U32 = mybir.dt.uint32
+U8 = mybir.dt.uint8
+FP8X4 = mybir.dt.float8_e4m3fn_x4
+
+P = 128
+ROWS = 2048
+HID = 2048
+D_IN = 1024
+TILES = 16
+FLOPS = 2 * ROWS * D_IN * HID
+
+
+def tile_edge_update_only_pa_kernel(tc, node_fts, edge_fts, Wt, out):
+    nc = tc.nc
+    node_flat = node_fts.flatten_outer_dims()
+    edge_flat = edge_fts.flatten_outer_dims()
+    out_flat = out.flatten_outer_dims()
+    edge_view = edge_flat.rearrange("(r m) c -> r (m c)", m=TILES)
+    wt_view = Wt.rearrange("(c q s) k -> q c (s k)", q=P, s=2)
+    out_view = out_flat.rearrange("(r m) h -> r m h", m=TILES)
+
+    with ExitStack() as ctx:
+        const = ctx.enter_context(tc.tile_pool(name="const", bufs=1))
+        stage = ctx.enter_context(tc.tile_pool(name="stage", bufs=3))
+        ypool = ctx.enter_context(tc.tile_pool(name="ypool", bufs=4))
+        opool = ctx.enter_context(tc.tile_pool(name="opool", bufs=4))
+        psum = ctx.enter_context(tc.psum_pool(name="psum", bufs=8))
+
+        node_sb = const.tile([P, 1024], BF16)
+        edge_sb = const.tile([P, 17 * 256], BF16)
+        wt_sb = const.tile([P, 8, 2048], BF16)
+        ident = const.tile([P, P], F32)
+        small_in = const.tile([P, 1024], BF16, align_bytes=64)
+        small_codes = const.tile([P, 256], U32, align_bytes=64)
+        small_plane = const.tile([P, 256], U8, align_bytes=64)
+        w_codes = const.tile([P, 2, HID], U32, align_bytes=64)
+        w_plane = const.tile([P, 2, HID], U8, align_bytes=64)
+        t_codes = [const.tile([P, ROWS], U32, align_bytes=64, name="t_codes%d" % g) for g in range(2)]
+        t_plane = [const.tile([P, ROWS], U8, align_bytes=64, name="t_plane%d" % g) for g in range(2)]
+
+        nc.vector.memset(node_sb[64:128, :], 0.0)
+        nc.vector.memset(node_sb[0:64, 768:1024], 0.0)
+        nc.vector.memset(edge_sb[:, 0:256], 0.0)
+        nc.vector.memset(small_plane[:].bitcast(I32), 0)
+        nc.sync.dma_start(out=node_sb[0:64, 0:384], in_=node_flat)
+        nc.sync.dma_start(out=node_sb[0:64, 384:768], in_=node_flat)
+        for half in range(2):
+            nc.sync.dma_start(
+                out=edge_sb[:, 256 + 2048 * half : 256 + 2048 * (half + 1)],
+                in_=edge_view[:, 2048 * half : 2048 * (half + 1)],
+            )
+        for c in range(8):
+            nc.sync.dma_start(out=wt_sb[:, c, :], in_=wt_view[:, c, :])
+        make_identity(nc, ident[:])
+
+        node32 = node_sb[:].bitcast(F32).rearrange("r (g w u) -> r g u w", g=2, w=P, u=2)
+        pn = psum.tile([P, 512], F32, tag="bank")
+        for g in range(2):
+            for u in range(2):
+                nc.tensor.transpose(pn[:, (2 * g + u) * P : (2 * g + u + 1) * P], node32[:, g, u, :], ident[:])
+        small32 = small_in[:].bitcast(F32)
+        nc.vector.tensor_copy(
+            out=small32[0:96, 0:256].rearrange("p (j rep u) -> p j rep u", j=64, rep=2, u=2),
+            in_=pn[0:96, 0:256]
+            .rearrange("p (u c) -> p c u", u=2)[:, 0:64, :]
+            .unsqueeze(2)
+            .to_broadcast([96, 64, 2, 2]),
+        )
+        for g, lo, hi in ((0, 96, 128), (1, 0, 128)):
+            dst_out = small32[lo:hi, 256 * g : 256 * (g + 1)].rearrange(
+                "p (m b rep kh u) -> p m b rep kh u", m=16, b=2, rep=2, kh=2, u=2
+            )
+            dst_in = pn[lo:hi, 256 * g : 256 * (g + 1)].rearrange(
+                "p (u z b kh m) -> p z b m kh u", u=2, z=2, b=2, kh=2, m=16
+            )
+            for b in range(2):
+                for rep in range(2):
+                    nc.vector.tensor_copy(out=dst_out[:, :, b, rep, :, :], in_=dst_in[:, 0, b, :, :, :])
+        nc.vector.quantize_mx(out=small_codes[:].bitcast(FP8X4), scales=small_plane[:], in_=small_in[:])
+
+        nc.vector.tensor_copy(
+            out=t_codes[0][0:96, :].bitcast(I32).rearrange("p (m r) -> p m r", m=TILES),
+            in_=small_codes[0:96, 0:128].bitcast(I32).unsqueeze(1).to_broadcast([96, TILES, 128]),
+        )
+        nc.vector.tensor_copy(
+            out=t_plane[0][0:96, :].bitcast(I32).rearrange("p (m w) -> p m w", m=TILES),
+            in_=small_plane[0:96, 0:128].bitcast(I32).unsqueeze(1).to_broadcast([96, TILES, 32]),
+        )
+        nc.vector.tensor_copy(
+            out=t_codes[0][96:128, :].bitcast(I32).rearrange("p (mb i x) -> p mb i x", mb=32, i=16, x=4),
+            in_=small_codes[96:128, 0:128]
+            .bitcast(I32)
+            .rearrange("p (mb x) -> p mb x", x=4)
+            .unsqueeze(2)
+            .to_broadcast([32, 32, 16, 4]),
+        )
+        nc.vector.tensor_copy(
+            out=t_plane[0][96:128, :].bitcast(I32).rearrange("p (mb w) -> p mb w", mb=32),
+            in_=small_plane[96:128, 0:128].bitcast(I32).unsqueeze(2).to_broadcast([32, 32, 16]),
+        )
+
+        edge32 = edge_sb[:].bitcast(F32).rearrange("r (x u) -> r u x", u=2)
+        for grp in range(4):
+            g1 = stage.tile([P, 2048], BF16, align_bytes=64, tag="g1")
+            g1_32 = g1[:].bitcast(F32)
+            for pair in range(2):
+                pe_bank = psum.tile([P, 512], F32, tag="bank")
+                for mm in range(2):
+                    m = 4 * grp + 2 * pair + mm
+                    for u in range(2):
+                        nc.tensor.transpose(
+                            pe_bank[:, (2 * mm + u) * P : (2 * mm + u + 1) * P],
+                            edge32[:, u, 64 * m : 64 * m + P],
+                            ident[:],
+                        )
+                nc.scalar.copy(
+                    out=g1_32[:, 512 * pair : 512 * (pair + 1)].rearrange("p (mm r u) -> p mm r u", mm=2, u=2),
+                    in_=pe_bank[:].rearrange("p (mm u r) -> p mm r u", mm=2, u=2),
+                )
+            cols = slice(512 * grp, 512 * (grp + 1))
+            nc.vector.quantize_mx(out=t_codes[1][:, cols].bitcast(FP8X4), scales=t_plane[1][:, cols], in_=g1[:])
+            nc.vector.tensor_copy(
+                out=t_codes[1][0:64, cols].bitcast(I32).rearrange("p (mb i x) -> p mb i x", mb=8, i=16, x=4),
+                in_=small_codes[0:64, 128 + 32 * grp : 128 + 32 * (grp + 1)]
+                .bitcast(I32)
+                .rearrange("p (mb x) -> p mb x", x=4)
+                .unsqueeze(2)
+                .to_broadcast([64, 8, 16, 4]),
+            )
+            nc.vector.tensor_copy(
+                out=t_plane[1][0:64, cols].bitcast(I32).rearrange("p (mb w) -> p mb w", mb=8),
+                in_=small_plane[0:64, 128 + 32 * grp : 128 + 32 * (grp + 1)]
+                .bitcast(I32)
+                .unsqueeze(2)
+                .to_broadcast([64, 8, 16]),
+            )
+
+        wt32 = wt_sb[:].bitcast(F32).rearrange("q c (s g w u) -> q c s g u w", s=2, g=2, w=P, u=2)
+        for cp in range(4):
+            for g in range(2):
+                gw = stage.tile([P, 2048], BF16, align_bytes=64, tag="gw")
+                gw32 = gw[:].bitcast(F32)
+                for half in range(2):
+                    c = 2 * cp + half
+                    pw = psum.tile([P, 512], F32, tag="bank")
+                    for s in range(2):
+                        for u in range(2):
+                            nc.tensor.transpose(
+                                pw[:, (2 * s + u) * P : (2 * s + u + 1) * P], wt32[:, c, s, g, u, :], ident[:]
+                            )
+                    nc.scalar.copy(
+                        out=gw32[:, 512 * half : 512 * (half + 1)].rearrange("p (q x) -> p q x", x=4),
+                        in_=pw[:].rearrange("p (x q) -> p q x", x=4),
+                    )
+                cols = slice(512 * cp, 512 * (cp + 1))
+                nc.vector.quantize_mx(out=w_codes[:, g, cols].bitcast(FP8X4), scales=w_plane[:, g, cols], in_=gw[:])
+
+        for m in range(TILES):
+            o = opool.tile([P, HID], F32, tag="o")
+            rows = slice(P * m, P * (m + 1))
+            for c4 in range(4):
+                cols = slice(512 * c4, 512 * (c4 + 1))
+                acc = psum.tile([P, 512], F32, tag="bank")
+                for g in range(2):
+                    nc.tensor.matmul_mx(
+                        out=acc[:],
+                        lhsT=t_codes[g][:, rows].bitcast(FP8X4),
+                        lhsT_scale=t_plane[g][:, rows],
+                        rhs=w_codes[:, g, cols].bitcast(FP8X4),
+                        rhs_scale=w_plane[:, g, cols],
+                        start=(g == 0),
+                        stop=(g == 1),
+                    )
+                y = ypool.tile([P, 512], F32, tag="y")
+                nc.scalar.mul(out=y[:], in_=acc[:], mul=0.1)
+                nc.vector.tensor_tensor(out=o[:, cols], in0=acc[:], in1=y[:], op=mybir.AluOpType.max)
+            nc.sync.dma_start(out=out_view[:, m, :], in_=o[:])

@@ -32,6 +32,8 @@ def tile_edge_update_only_pa_kernel(tc, node_fts, edge_fts, Wt, out):
         stage = ctx.enter_context(tc.tile_pool(name="stage", bufs=3))
         ypool = ctx.enter_context(tc.tile_pool(name="ypool", bufs=4))
         opool = ctx.enter_context(tc.tile_pool(name="opool", bufs=4))
+        xpool = ctx.enter_context(tc.tile_pool(name="xpool", bufs=3))
+        fpool = ctx.enter_context(tc.tile_pool(name="fpool", bufs=2))
         psum = ctx.enter_context(tc.psum_pool(name="psum", bufs=8))
 
         node_sb = const.tile([P, 1024], BF16)
@@ -52,14 +54,14 @@ def tile_edge_update_only_pa_kernel(tc, node_fts, edge_fts, Wt, out):
         nc.vector.memset(small_plane[:].bitcast(I32), 0)
         nc.sync.dma_start(out=node_sb[0:64, 0:384], in_=node_flat)
         nc.sync.dma_start(out=node_sb[0:64, 384:768], in_=node_flat)
-        for half in range(2):
-            nc.sync.dma_start(
-                out=edge_sb[:, 256 + 2048 * half : 256 + 2048 * (half + 1)],
-                in_=edge_view[:, 2048 * half : 2048 * (half + 1)],
-            )
+        nc.sync.dma_start(out=edge_sb[:, 256:1280], in_=edge_view[:, 0:1024])
         for c in range(8):
             nc.sync.dma_start(out=wt_sb[:, c, :], in_=wt_view[:, c, :])
+        nc.sync.dma_start(out=edge_sb[:, 1280:4352], in_=edge_view[:, 1024:4096])
         make_identity(nc, ident[:])
+        warm = const.tile([P, 8], F32)
+        nc.vector.memset(warm[:], 0.0)
+        nc.scalar.mul(out=warm[:, 0:4], in_=warm[:, 4:8], mul=0.1)
 
         node32 = node_sb[:].bitcast(F32).rearrange("r (g w u) -> r g u w", g=2, w=P, u=2)
         pn = psum.tile([P, 512], F32, tag="bank")
@@ -108,7 +110,7 @@ def tile_edge_update_only_pa_kernel(tc, node_fts, edge_fts, Wt, out):
         )
 
         edge32 = edge_sb[:].bitcast(F32).rearrange("r (x u) -> r u x", u=2)
-        for grp in range(4):
+        def edge_group(grp):
             g1 = stage.tile([P, 2048], BF16, align_bytes=64, tag="g1")
             g1_32 = g1[:].bitcast(F32)
             for pair in range(2):
@@ -143,6 +145,8 @@ def tile_edge_update_only_pa_kernel(tc, node_fts, edge_fts, Wt, out):
                 .to_broadcast([64, 8, 16]),
             )
 
+        edge_group(0)
+
         wt32 = wt_sb[:].bitcast(F32).rearrange("q c (s g w u) -> q c s g u w", s=2, g=2, w=P, u=2)
         for cp in range(4):
             for g in range(2):
@@ -166,6 +170,7 @@ def tile_edge_update_only_pa_kernel(tc, node_fts, edge_fts, Wt, out):
         for m in range(TILES):
             o = opool.tile([P, HID], F32, tag="o")
             rows = slice(P * m, P * (m + 1))
+            last = m == TILES - 1
             for c4 in range(4):
                 cols = slice(512 * c4, 512 * (c4 + 1))
                 acc = psum.tile([P, 512], F32, tag="bank")
@@ -179,7 +184,25 @@ def tile_edge_update_only_pa_kernel(tc, node_fts, edge_fts, Wt, out):
                         start=(g == 0),
                         stop=(g == 1),
                     )
-                y = ypool.tile([P, 512], F32, tag="y")
-                nc.scalar.mul(out=y[:], in_=acc[:], mul=0.1)
-                nc.vector.tensor_tensor(out=o[:, cols], in0=acc[:], in1=y[:], op=mybir.AluOpType.max)
-            nc.sync.dma_start(out=out_view[:, m, :], in_=o[:])
+                if c4 == 0 and not last:
+                    xs = xpool.tile([P, 512], F32, tag="xs")
+                    if m % 2 == 0:
+                        nc.scalar.copy(out=xs[:], in_=acc[:])
+                    else:
+                        nc.vector.tensor_copy(out=xs[:], in_=acc[:])
+                    f = fpool.tile([P, 512], F32, tag="f")
+                    nc.gpsimd.tensor_scalar(
+                        out=f[:], in0=xs[:], scalar1=0.0, scalar2=0.1,
+                        op0=mybir.AluOpType.is_ge, op1=mybir.AluOpType.max,
+                    )
+                    nc.gpsimd.tensor_tensor(out=o[:, cols], in0=f[:], in1=xs[:], op=mybir.AluOpType.mult)
+                else:
+                    y = ypool.tile([P, 512], F32, tag="y")
+                    nc.scalar.mul(out=y[:], in_=acc[:], mul=0.1)
+                    nc.vector.tensor_tensor(out=o[:, cols], in0=acc[:], in1=y[:], op=mybir.AluOpType.max)
+                if last:
+                    nc.sync.dma_start(out=out_view[:, m, cols], in_=o[:, cols])
+            if not last:
+                nc.sync.dma_start(out=out_view[:, m, :], in_=o[:])
+            if m in (1, 5, 9):
+                edge_group((m + 3) // 4)

@@ -16,6 +16,7 @@ HID = 2048
 D_IN = 1024
 TILES = 16
 FLOPS = 2 * ROWS * D_IN * HID
+PIN = True
 
 
 def tile_edge_update_only_pa_kernel(tc, node_fts, edge_fts, Wt, out):
@@ -31,9 +32,9 @@ def tile_edge_update_only_pa_kernel(tc, node_fts, edge_fts, Wt, out):
         const = ctx.enter_context(tc.tile_pool(name="const", bufs=1))
         stage = ctx.enter_context(tc.tile_pool(name="stage", bufs=3))
         ypool = ctx.enter_context(tc.tile_pool(name="ypool", bufs=4))
-        opool = ctx.enter_context(tc.tile_pool(name="opool", bufs=4))
-        xpool = ctx.enter_context(tc.tile_pool(name="xpool", bufs=3))
-        fpool = ctx.enter_context(tc.tile_pool(name="fpool", bufs=2))
+        opool = ctx.enter_context(tc.tile_pool(name="opool", bufs=6))
+        if PIN:
+            ctx.enter_context(tc.manual_schedule())
         psum = ctx.enter_context(tc.psum_pool(name="psum", bufs=8))
 
         node_sb = const.tile([P, 1024], BF16)
@@ -55,9 +56,11 @@ def tile_edge_update_only_pa_kernel(tc, node_fts, edge_fts, Wt, out):
         nc.sync.dma_start(out=node_sb[0:64, 0:384], in_=node_flat)
         nc.sync.dma_start(out=node_sb[0:64, 384:768], in_=node_flat)
         nc.sync.dma_start(out=edge_sb[:, 256:1280], in_=edge_view[:, 0:1024])
-        for c in range(8):
+        for c in range(4):
             nc.sync.dma_start(out=wt_sb[:, c, :], in_=wt_view[:, c, :])
         nc.sync.dma_start(out=edge_sb[:, 1280:4352], in_=edge_view[:, 1024:4096])
+        for c in range(4, 8):
+            nc.sync.dma_start(out=wt_sb[:, c, :], in_=wt_view[:, c, :])
         make_identity(nc, ident[:])
         warm = const.tile([P, 8], F32)
         nc.vector.memset(warm[:], 0.0)
@@ -88,26 +91,31 @@ def tile_edge_update_only_pa_kernel(tc, node_fts, edge_fts, Wt, out):
                     nc.vector.tensor_copy(out=dst_out[:, :, b, rep, :, :], in_=dst_in[:, 0, b, :, :, :])
         nc.vector.quantize_mx(out=small_codes[:].bitcast(FP8X4), scales=small_plane[:], in_=small_in[:])
 
-        nc.vector.tensor_copy(
-            out=t_codes[0][0:96, :].bitcast(I32).rearrange("p (m r) -> p m r", m=TILES),
-            in_=small_codes[0:96, 0:128].bitcast(I32).unsqueeze(1).to_broadcast([96, TILES, 128]),
-        )
-        nc.vector.tensor_copy(
-            out=t_plane[0][0:96, :].bitcast(I32).rearrange("p (m w) -> p m w", m=TILES),
-            in_=small_plane[0:96, 0:128].bitcast(I32).unsqueeze(1).to_broadcast([96, TILES, 32]),
-        )
-        nc.vector.tensor_copy(
-            out=t_codes[0][96:128, :].bitcast(I32).rearrange("p (mb i x) -> p mb i x", mb=32, i=16, x=4),
-            in_=small_codes[96:128, 0:128]
-            .bitcast(I32)
-            .rearrange("p (mb x) -> p mb x", x=4)
-            .unsqueeze(2)
-            .to_broadcast([32, 32, 16, 4]),
-        )
-        nc.vector.tensor_copy(
-            out=t_plane[0][96:128, :].bitcast(I32).rearrange("p (mb w) -> p mb w", mb=32),
-            in_=small_plane[96:128, 0:128].bitcast(I32).unsqueeze(2).to_broadcast([32, 32, 16]),
-        )
+        def pass0_tiles(m_lo, m_hi):
+            n = m_hi - m_lo
+            cols = slice(P * m_lo, P * m_hi)
+            nc.vector.tensor_copy(
+                out=t_codes[0][0:96, cols].bitcast(I32).rearrange("p (m r) -> p m r", m=n),
+                in_=small_codes[0:96, 0:128].bitcast(I32).unsqueeze(1).to_broadcast([96, n, 128]),
+            )
+            nc.vector.tensor_copy(
+                out=t_plane[0][0:96, cols].bitcast(I32).rearrange("p (m w) -> p m w", m=n),
+                in_=small_plane[0:96, 0:128].bitcast(I32).unsqueeze(1).to_broadcast([96, n, 32]),
+            )
+            nc.vector.tensor_copy(
+                out=t_codes[0][96:128, cols].bitcast(I32).rearrange("p (mb i x) -> p mb i x", mb=2 * n, i=16, x=4),
+                in_=small_codes[96:128, 8 * m_lo : 8 * m_hi]
+                .bitcast(I32)
+                .rearrange("p (mb x) -> p mb x", x=4)
+                .unsqueeze(2)
+                .to_broadcast([32, 2 * n, 16, 4]),
+            )
+            nc.vector.tensor_copy(
+                out=t_plane[0][96:128, cols].bitcast(I32).rearrange("p (mb w) -> p mb w", mb=2 * n),
+                in_=small_plane[96:128, 8 * m_lo : 8 * m_hi].bitcast(I32).unsqueeze(2).to_broadcast([32, 2 * n, 16]),
+            )
+
+        pass0_tiles(0, 4)
 
         edge32 = edge_sb[:].bitcast(F32).rearrange("r (x u) -> r u x", u=2)
         def edge_group(grp):
@@ -148,61 +156,60 @@ def tile_edge_update_only_pa_kernel(tc, node_fts, edge_fts, Wt, out):
         edge_group(0)
 
         wt32 = wt_sb[:].bitcast(F32).rearrange("q c (s g w u) -> q c s g u w", s=2, g=2, w=P, u=2)
-        for cp in range(4):
-            for g in range(2):
-                gw = stage.tile([P, 2048], BF16, align_bytes=64, tag="gw")
-                gw32 = gw[:].bitcast(F32)
-                for half in range(2):
-                    c = 2 * cp + half
-                    pw = psum.tile([P, 512], F32, tag="bank")
-                    for s in range(2):
-                        for u in range(2):
-                            nc.tensor.transpose(
-                                pw[:, (2 * s + u) * P : (2 * s + u + 1) * P], wt32[:, c, s, g, u, :], ident[:]
-                            )
-                    nc.scalar.copy(
-                        out=gw32[:, 512 * half : 512 * (half + 1)].rearrange("p (q x) -> p q x", x=4),
-                        in_=pw[:].rearrange("p (x q) -> p q x", x=4),
-                    )
-                cols = slice(512 * cp, 512 * (cp + 1))
-                nc.vector.quantize_mx(out=w_codes[:, g, cols].bitcast(FP8X4), scales=w_plane[:, g, cols], in_=gw[:])
 
-        for m in range(TILES):
-            o = opool.tile([P, HID], F32, tag="o")
-            rows = slice(P * m, P * (m + 1))
-            last = m == TILES - 1
-            for c4 in range(4):
-                cols = slice(512 * c4, 512 * (c4 + 1))
-                acc = psum.tile([P, 512], F32, tag="bank")
-                for g in range(2):
-                    nc.tensor.matmul_mx(
-                        out=acc[:],
-                        lhsT=t_codes[g][:, rows].bitcast(FP8X4),
-                        lhsT_scale=t_plane[g][:, rows],
-                        rhs=w_codes[:, g, cols].bitcast(FP8X4),
-                        rhs_scale=w_plane[:, g, cols],
-                        start=(g == 0),
-                        stop=(g == 1),
-                    )
-                if c4 == 0 and not last:
-                    xs = xpool.tile([P, 512], F32, tag="xs")
-                    if m % 2 == 0:
-                        nc.scalar.copy(out=xs[:], in_=acc[:])
-                    else:
-                        nc.vector.tensor_copy(out=xs[:], in_=acc[:])
-                    f = fpool.tile([P, 512], F32, tag="f")
-                    nc.gpsimd.tensor_scalar(
-                        out=f[:], in0=xs[:], scalar1=0.0, scalar2=0.1,
-                        op0=mybir.AluOpType.is_ge, op1=mybir.AluOpType.max,
-                    )
-                    nc.gpsimd.tensor_tensor(out=o[:, cols], in0=f[:], in1=xs[:], op=mybir.AluOpType.mult)
-                else:
+        def weight_unit(cp, g):
+            gw = stage.tile([P, 2048], BF16, align_bytes=64, tag="gw")
+            gw32 = gw[:].bitcast(F32)
+            for half in range(2):
+                c = 2 * cp + half
+                pw = psum.tile([P, 512], F32, tag="bank")
+                for s in range(2):
+                    for u in range(2):
+                        nc.tensor.transpose(
+                            pw[:, (2 * s + u) * P : (2 * s + u + 1) * P], wt32[:, c, s, g, u, :], ident[:]
+                        )
+                nc.scalar.copy(
+                    out=gw32[:, 512 * half : 512 * (half + 1)].rearrange("p (q x) -> p q x", x=4),
+                    in_=pw[:].rearrange("p (x q) -> p q x", x=4),
+                )
+            cols = slice(512 * cp, 512 * (cp + 1))
+            nc.vector.quantize_mx(out=w_codes[:, g, cols].bitcast(FP8X4), scales=w_plane[:, g, cols], in_=gw[:])
+
+        for cp in range(2):
+            for g in range(2):
+                weight_unit(cp, g)
+
+        for hh in range(2):
+            for m in range(TILES):
+                o = opool.tile([P, 1024], F32, tag="o")
+                rows = slice(P * m, P * (m + 1))
+                last = hh == 1 and m == TILES - 1
+                for cc in range(2):
+                    cols = slice(1024 * hh + 512 * cc, 1024 * hh + 512 * (cc + 1))
+                    acc = psum.tile([P, 512], F32, tag="bank")
+                    for g in range(2):
+                        nc.tensor.matmul_mx(
+                            out=acc[:],
+                            lhsT=t_codes[g][:, rows].bitcast(FP8X4),
+                            lhsT_scale=t_plane[g][:, rows],
+                            rhs=w_codes[:, g, cols].bitcast(FP8X4),
+                            rhs_scale=w_plane[:, g, cols],
+                            start=(g == 0),
+                            stop=(g == 1),
+                        )
                     y = ypool.tile([P, 512], F32, tag="y")
                     nc.scalar.mul(out=y[:], in_=acc[:], mul=0.1)
-                    nc.vector.tensor_tensor(out=o[:, cols], in0=acc[:], in1=y[:], op=mybir.AluOpType.max)
-                if last:
-                    nc.sync.dma_start(out=out_view[:, m, cols], in_=o[:, cols])
-            if not last:
-                nc.sync.dma_start(out=out_view[:, m, :], in_=o[:])
-            if m in (1, 5, 9):
-                edge_group((m + 3) // 4)
+                    ocols = slice(512 * cc, 512 * (cc + 1))
+                    nc.vector.tensor_tensor(out=o[:, ocols], in0=acc[:], in1=y[:], op=mybir.AluOpType.max)
+                    if last:
+                        nc.sync.dma_start(out=out_view[:, m, cols], in_=o[:, ocols])
+                if not last:
+                    nc.sync.dma_start(out=out_view[:, m, 1024 * hh : 1024 * (hh + 1)], in_=o[:])
+                if hh == 0 and m % 2 == 1:
+                    step = m // 2
+                    if step == 0:
+                        pass0_tiles(4, TILES)
+                    if step < 3:
+                        edge_group(step + 1)
+                    elif step < 7:
+                        weight_unit(2 + (step - 3) // 2, (step - 3) % 2)

@@ -16,7 +16,6 @@ HID = 2048
 D_IN = 1024
 TILES = 16
 FLOPS = 2 * ROWS * D_IN * HID
-PIN = True
 
 
 def tile_edge_update_only_pa_kernel(tc, node_fts, edge_fts, Wt, out):
@@ -33,8 +32,6 @@ def tile_edge_update_only_pa_kernel(tc, node_fts, edge_fts, Wt, out):
         stage = ctx.enter_context(tc.tile_pool(name="stage", bufs=3))
         ypool = ctx.enter_context(tc.tile_pool(name="ypool", bufs=4))
         opool = ctx.enter_context(tc.tile_pool(name="opool", bufs=6))
-        if PIN:
-            ctx.enter_context(tc.manual_schedule())
         psum = ctx.enter_context(tc.psum_pool(name="psum", bufs=8))
 
         node_sb = const.tile([P, 1024], BF16)
@@ -55,16 +52,14 @@ def tile_edge_update_only_pa_kernel(tc, node_fts, edge_fts, Wt, out):
         nc.vector.memset(small_plane[:].bitcast(I32), 0)
         nc.sync.dma_start(out=node_sb[0:64, 0:384], in_=node_flat)
         nc.sync.dma_start(out=node_sb[0:64, 384:768], in_=node_flat)
-        nc.sync.dma_start(out=edge_sb[:, 256:1280], in_=edge_view[:, 0:1024])
-        for c in range(4):
-            nc.sync.dma_start(out=wt_sb[:, c, :], in_=wt_view[:, c, :])
-        nc.sync.dma_start(out=edge_sb[:, 1280:4352], in_=edge_view[:, 1024:4096])
-        for c in range(4, 8):
+        for half in range(2):
+            nc.sync.dma_start(
+                out=edge_sb[:, 256 + 2048 * half : 256 + 2048 * (half + 1)],
+                in_=edge_view[:, 2048 * half : 2048 * (half + 1)],
+            )
+        for c in range(8):
             nc.sync.dma_start(out=wt_sb[:, c, :], in_=wt_view[:, c, :])
         make_identity(nc, ident[:])
-        warm = const.tile([P, 8], F32)
-        nc.vector.memset(warm[:], 0.0)
-        nc.scalar.mul(out=warm[:, 0:4], in_=warm[:, 4:8], mul=0.1)
 
         node32 = node_sb[:].bitcast(F32).rearrange("r (g w u) -> r g u w", g=2, w=P, u=2)
         pn = psum.tile([P, 512], F32, tag="bank")
@@ -72,7 +67,7 @@ def tile_edge_update_only_pa_kernel(tc, node_fts, edge_fts, Wt, out):
             for u in range(2):
                 nc.tensor.transpose(pn[:, (2 * g + u) * P : (2 * g + u + 1) * P], node32[:, g, u, :], ident[:])
         small32 = small_in[:].bitcast(F32)
-        nc.vector.tensor_copy(
+        nc.scalar.copy(
             out=small32[0:96, 0:256].rearrange("p (j rep u) -> p j rep u", j=64, rep=2, u=2),
             in_=pn[0:96, 0:256]
             .rearrange("p (u c) -> p c u", u=2)[:, 0:64, :]
@@ -88,37 +83,32 @@ def tile_edge_update_only_pa_kernel(tc, node_fts, edge_fts, Wt, out):
             )
             for b in range(2):
                 for rep in range(2):
-                    nc.vector.tensor_copy(out=dst_out[:, :, b, rep, :, :], in_=dst_in[:, 0, b, :, :, :])
+                    nc.scalar.copy(out=dst_out[:, :, b, rep, :, :], in_=dst_in[:, 0, b, :, :, :])
         nc.vector.quantize_mx(out=small_codes[:].bitcast(FP8X4), scales=small_plane[:], in_=small_in[:])
 
-        def pass0_tiles(m_lo, m_hi):
-            n = m_hi - m_lo
-            cols = slice(P * m_lo, P * m_hi)
-            nc.vector.tensor_copy(
-                out=t_codes[0][0:96, cols].bitcast(I32).rearrange("p (m r) -> p m r", m=n),
-                in_=small_codes[0:96, 0:128].bitcast(I32).unsqueeze(1).to_broadcast([96, n, 128]),
-            )
-            nc.vector.tensor_copy(
-                out=t_plane[0][0:96, cols].bitcast(I32).rearrange("p (m w) -> p m w", m=n),
-                in_=small_plane[0:96, 0:128].bitcast(I32).unsqueeze(1).to_broadcast([96, n, 32]),
-            )
-            nc.vector.tensor_copy(
-                out=t_codes[0][96:128, cols].bitcast(I32).rearrange("p (mb i x) -> p mb i x", mb=2 * n, i=16, x=4),
-                in_=small_codes[96:128, 8 * m_lo : 8 * m_hi]
-                .bitcast(I32)
-                .rearrange("p (mb x) -> p mb x", x=4)
-                .unsqueeze(2)
-                .to_broadcast([32, 2 * n, 16, 4]),
-            )
-            nc.vector.tensor_copy(
-                out=t_plane[0][96:128, cols].bitcast(I32).rearrange("p (mb w) -> p mb w", mb=2 * n),
-                in_=small_plane[96:128, 8 * m_lo : 8 * m_hi].bitcast(I32).unsqueeze(2).to_broadcast([32, 2 * n, 16]),
-            )
-
-        pass0_tiles(0, 4)
+        nc.vector.tensor_copy(
+            out=t_codes[0][0:96, :].bitcast(I32).rearrange("p (m r) -> p m r", m=TILES),
+            in_=small_codes[0:96, 0:128].bitcast(I32).unsqueeze(1).to_broadcast([96, TILES, 128]),
+        )
+        nc.vector.tensor_copy(
+            out=t_plane[0][0:96, :].bitcast(I32).rearrange("p (m w) -> p m w", m=TILES),
+            in_=small_plane[0:96, 0:128].bitcast(I32).unsqueeze(1).to_broadcast([96, TILES, 32]),
+        )
+        nc.vector.tensor_copy(
+            out=t_codes[0][96:128, :].bitcast(I32).rearrange("p (mb i x) -> p mb i x", mb=32, i=16, x=4),
+            in_=small_codes[96:128, 0:128]
+            .bitcast(I32)
+            .rearrange("p (mb x) -> p mb x", x=4)
+            .unsqueeze(2)
+            .to_broadcast([32, 32, 16, 4]),
+        )
+        nc.vector.tensor_copy(
+            out=t_plane[0][96:128, :].bitcast(I32).rearrange("p (mb w) -> p mb w", mb=32),
+            in_=small_plane[96:128, 0:128].bitcast(I32).unsqueeze(2).to_broadcast([32, 32, 16]),
+        )
 
         edge32 = edge_sb[:].bitcast(F32).rearrange("r (x u) -> r u x", u=2)
-        def edge_group(grp):
+        for grp in range(4):
             g1 = stage.tile([P, 2048], BF16, align_bytes=64, tag="g1")
             g1_32 = g1[:].bitcast(F32)
             for pair in range(2):
@@ -137,53 +127,43 @@ def tile_edge_update_only_pa_kernel(tc, node_fts, edge_fts, Wt, out):
                 )
             cols = slice(512 * grp, 512 * (grp + 1))
             nc.vector.quantize_mx(out=t_codes[1][:, cols].bitcast(FP8X4), scales=t_plane[1][:, cols], in_=g1[:])
-            nc.vector.tensor_copy(
-                out=t_codes[1][0:64, cols].bitcast(I32).rearrange("p (mb i x) -> p mb i x", mb=8, i=16, x=4),
-                in_=small_codes[0:64, 128 + 32 * grp : 128 + 32 * (grp + 1)]
-                .bitcast(I32)
-                .rearrange("p (mb x) -> p mb x", x=4)
-                .unsqueeze(2)
-                .to_broadcast([64, 8, 16, 4]),
-            )
-            nc.vector.tensor_copy(
-                out=t_plane[1][0:64, cols].bitcast(I32).rearrange("p (mb w) -> p mb w", mb=8),
-                in_=small_plane[0:64, 128 + 32 * grp : 128 + 32 * (grp + 1)]
-                .bitcast(I32)
-                .unsqueeze(2)
-                .to_broadcast([64, 8, 16]),
-            )
-
-        edge_group(0)
+        nc.vector.tensor_copy(
+            out=t_codes[1][0:64, :].bitcast(I32).rearrange("p (mb i x) -> p mb i x", mb=32, i=16, x=4),
+            in_=small_codes[0:64, 128:256]
+            .bitcast(I32)
+            .rearrange("p (mb x) -> p mb x", x=4)
+            .unsqueeze(2)
+            .to_broadcast([64, 32, 16, 4]),
+        )
+        nc.vector.tensor_copy(
+            out=t_plane[1][0:64, :].bitcast(I32).rearrange("p (mb w) -> p mb w", mb=32),
+            in_=small_plane[0:64, 128:256].bitcast(I32).unsqueeze(2).to_broadcast([64, 32, 16]),
+        )
 
         wt32 = wt_sb[:].bitcast(F32).rearrange("q c (s g w u) -> q c s g u w", s=2, g=2, w=P, u=2)
-
-        def weight_unit(cp, g):
-            gw = stage.tile([P, 2048], BF16, align_bytes=64, tag="gw")
-            gw32 = gw[:].bitcast(F32)
-            for half in range(2):
-                c = 2 * cp + half
-                pw = psum.tile([P, 512], F32, tag="bank")
-                for s in range(2):
-                    for u in range(2):
-                        nc.tensor.transpose(
-                            pw[:, (2 * s + u) * P : (2 * s + u + 1) * P], wt32[:, c, s, g, u, :], ident[:]
-                        )
-                nc.scalar.copy(
-                    out=gw32[:, 512 * half : 512 * (half + 1)].rearrange("p (q x) -> p q x", x=4),
-                    in_=pw[:].rearrange("p (x q) -> p q x", x=4),
-                )
-            cols = slice(512 * cp, 512 * (cp + 1))
-            nc.vector.quantize_mx(out=w_codes[:, g, cols].bitcast(FP8X4), scales=w_plane[:, g, cols], in_=gw[:])
-
-        for cp in range(2):
+        for cp in range(4):
             for g in range(2):
-                weight_unit(cp, g)
+                gw = stage.tile([P, 2048], BF16, align_bytes=64, tag="gw")
+                gw32 = gw[:].bitcast(F32)
+                for half in range(2):
+                    c = 2 * cp + half
+                    pw = psum.tile([P, 512], F32, tag="bank")
+                    for s in range(2):
+                        for u in range(2):
+                            nc.tensor.transpose(
+                                pw[:, (2 * s + u) * P : (2 * s + u + 1) * P], wt32[:, c, s, g, u, :], ident[:]
+                            )
+                    nc.scalar.copy(
+                        out=gw32[:, 512 * half : 512 * (half + 1)].rearrange("p (q x) -> p q x", x=4),
+                        in_=pw[:].rearrange("p (x q) -> p q x", x=4),
+                    )
+                cols = slice(512 * cp, 512 * (cp + 1))
+                nc.vector.quantize_mx(out=w_codes[:, g, cols].bitcast(FP8X4), scales=w_plane[:, g, cols], in_=gw[:])
 
-        for hh in range(2):
-            for m in range(TILES):
+        for m in range(TILES):
+            rows = slice(P * m, P * (m + 1))
+            for hh in range(2):
                 o = opool.tile([P, 1024], F32, tag="o")
-                rows = slice(P * m, P * (m + 1))
-                last = hh == 1 and m == TILES - 1
                 for cc in range(2):
                     cols = slice(1024 * hh + 512 * cc, 1024 * hh + 512 * (cc + 1))
                     acc = psum.tile([P, 512], F32, tag="bank")
@@ -198,18 +178,13 @@ def tile_edge_update_only_pa_kernel(tc, node_fts, edge_fts, Wt, out):
                             stop=(g == 1),
                         )
                     y = ypool.tile([P, 512], F32, tag="y")
-                    nc.scalar.mul(out=y[:], in_=acc[:], mul=0.1)
-                    ocols = slice(512 * cc, 512 * (cc + 1))
-                    nc.vector.tensor_tensor(out=o[:, ocols], in0=acc[:], in1=y[:], op=mybir.AluOpType.max)
-                    if last:
-                        nc.sync.dma_start(out=out_view[:, m, cols], in_=o[:, ocols])
-                if not last:
-                    nc.sync.dma_start(out=out_view[:, m, 1024 * hh : 1024 * (hh + 1)], in_=o[:])
-                if hh == 0 and m % 2 == 1:
-                    step = m // 2
-                    if step == 0:
-                        pass0_tiles(4, TILES)
-                    if step < 3:
-                        edge_group(step + 1)
-                    elif step < 7:
-                        weight_unit(2 + (step - 3) // 2, (step - 3) % 2)
+                    nc.scalar.copy(out=y[:], in_=acc[:])
+                    nc.vector.scalar_tensor_tensor(
+                        out=o[:, 512 * cc : 512 * (cc + 1)],
+                        in0=acc[:],
+                        scalar=0.1,
+                        in1=y[:],
+                        op0=mybir.AluOpType.mult,
+                        op1=mybir.AluOpType.max,
+                    )
+                nc.sync.dma_start(out=out_view[:, m, 1024 * hh : 1024 * (hh + 1)], in_=o[:])

@@ -29,15 +29,18 @@ def tile_edge_update_only_pa_kernel(tc, node_fts, edge_fts, Wt, out):
 
     with ExitStack() as ctx:
         const = ctx.enter_context(tc.tile_pool(name="const", bufs=1))
-        stage = ctx.enter_context(tc.tile_pool(name="stage", bufs=3))
+        stage = ctx.enter_context(tc.tile_pool(name="stage", bufs=4))
         ypool = ctx.enter_context(tc.tile_pool(name="ypool", bufs=4))
         opool = ctx.enter_context(tc.tile_pool(name="opool", bufs=6))
+        gpool = ctx.enter_context(tc.tile_pool(name="gpool", bufs=2))
         psum = ctx.enter_context(tc.psum_pool(name="psum", bufs=8))
+        ctx.enter_context(tc.manual_schedule(engines={mybir.EngineType.Pool}))
 
         node_sb = const.tile([P, 1024], BF16)
         edge_sb = const.tile([P, 17 * 256], BF16)
         wt_sb = const.tile([P, 8, 2048], BF16)
         ident = const.tile([P, P], F32)
+        warm_sb = const.tile([P, 512], BF16)
         small_in = const.tile([P, 1024], BF16, align_bytes=64)
         small_codes = const.tile([P, 256], U32, align_bytes=64)
         small_plane = const.tile([P, 256], U8, align_bytes=64)
@@ -46,69 +49,108 @@ def tile_edge_update_only_pa_kernel(tc, node_fts, edge_fts, Wt, out):
         t_codes = [const.tile([P, ROWS], U32, align_bytes=64, name="t_codes%d" % g) for g in range(2)]
         t_plane = [const.tile([P, ROWS], U8, align_bytes=64, name="t_plane%d" % g) for g in range(2)]
 
+        nc.vector.memset(warm_sb[:], 0.0)
         nc.vector.memset(node_sb[64:128, :], 0.0)
         nc.vector.memset(node_sb[0:64, 768:1024], 0.0)
         nc.vector.memset(edge_sb[:, 0:256], 0.0)
         nc.vector.memset(small_plane[:].bitcast(I32), 0)
-        nc.sync.dma_start(out=node_sb[0:64, 0:384], in_=node_flat)
-        nc.sync.dma_start(out=node_sb[0:64, 384:768], in_=node_flat)
-        for half in range(2):
-            nc.sync.dma_start(
-                out=edge_sb[:, 256 + 2048 * half : 256 + 2048 * (half + 1)],
-                in_=edge_view[:, 2048 * half : 2048 * (half + 1)],
-            )
-        for c in range(8):
+        def load_node():
+            nc.sync.dma_start(out=node_sb[0:64, 0:384], in_=node_flat)
+            nc.sync.dma_start(out=node_sb[0:64, 384:768], in_=node_flat)
+
+        def load_edge(t0, t1):
+            nc.sync.dma_start(out=edge_sb[:, 256 + 256 * t0 : 256 + 256 * t1], in_=edge_view[:, 256 * t0 : 256 * t1])
+
+        def load_w(c):
             nc.sync.dma_start(out=wt_sb[:, c, :], in_=wt_view[:, c, :])
+
+        load_node()
+        load_edge(0, 8)
+        load_edge(8, 16)
+        for c in range(8):
+            load_w(c)
         make_identity(nc, ident[:])
 
-        node32 = node_sb[:].bitcast(F32).rearrange("r (g w u) -> r g u w", g=2, w=P, u=2)
-        pn = psum.tile([P, 512], F32, tag="bank")
-        for g in range(2):
-            for u in range(2):
-                nc.tensor.transpose(pn[:, (2 * g + u) * P : (2 * g + u + 1) * P], node32[:, g, u, :], ident[:])
-        small32 = small_in[:].bitcast(F32)
-        nc.scalar.copy(
-            out=small32[0:96, 0:256].rearrange("p (j rep u) -> p j rep u", j=64, rep=2, u=2),
-            in_=pn[0:96, 0:256]
-            .rearrange("p (u c) -> p c u", u=2)[:, 0:64, :]
-            .unsqueeze(2)
-            .to_broadcast([96, 64, 2, 2]),
-        )
-        for g, lo, hi in ((0, 96, 128), (1, 0, 128)):
-            dst_out = small32[lo:hi, 256 * g : 256 * (g + 1)].rearrange(
-                "p (m b rep kh u) -> p m b rep kh u", m=16, b=2, rep=2, kh=2, u=2
-            )
-            dst_in = pn[lo:hi, 256 * g : 256 * (g + 1)].rearrange(
-                "p (u z b kh m) -> p z b m kh u", u=2, z=2, b=2, kh=2, m=16
-            )
-            for b in range(2):
-                for rep in range(2):
-                    nc.scalar.copy(out=dst_out[:, :, b, rep, :, :], in_=dst_in[:, 0, b, :, :, :])
-        nc.vector.quantize_mx(out=small_codes[:].bitcast(FP8X4), scales=small_plane[:], in_=small_in[:])
+        def warm(n):
+            for i in range(n):
+                wp = psum.tile([P, 512], F32, tag="bank")
+                nc.tensor.matmul(out=wp[:], lhsT=warm_sb[:, 0:P], rhs=warm_sb[:], start=True, stop=True)
 
-        nc.vector.tensor_copy(
-            out=t_codes[0][0:96, :].bitcast(I32).rearrange("p (m r) -> p m r", m=TILES),
-            in_=small_codes[0:96, 0:128].bitcast(I32).unsqueeze(1).to_broadcast([96, TILES, 128]),
-        )
-        nc.vector.tensor_copy(
-            out=t_plane[0][0:96, :].bitcast(I32).rearrange("p (m w) -> p m w", m=TILES),
-            in_=small_plane[0:96, 0:128].bitcast(I32).unsqueeze(1).to_broadcast([96, TILES, 32]),
-        )
-        nc.vector.tensor_copy(
-            out=t_codes[0][96:128, :].bitcast(I32).rearrange("p (mb i x) -> p mb i x", mb=32, i=16, x=4),
-            in_=small_codes[96:128, 0:128]
-            .bitcast(I32)
-            .rearrange("p (mb x) -> p mb x", x=4)
-            .unsqueeze(2)
-            .to_broadcast([32, 32, 16, 4]),
-        )
-        nc.vector.tensor_copy(
-            out=t_plane[0][96:128, :].bitcast(I32).rearrange("p (mb w) -> p mb w", mb=32),
-            in_=small_plane[96:128, 0:128].bitcast(I32).unsqueeze(2).to_broadcast([32, 32, 16]),
-        )
+        def bank_copy(eng, dst, src):
+            if eng == "v":
+                nc.vector.tensor_copy(out=dst, in_=src)
+            else:
+                nc.scalar.copy(out=dst, in_=src)
+
+        def node_prep():
+            node32 = node_sb[:].bitcast(F32).rearrange("r (g w u) -> r g u w", g=2, w=P, u=2)
+            pn = psum.tile([P, 512], F32, tag="bank")
+            for g in range(2):
+                for u in range(2):
+                    nc.tensor.transpose(pn[:, (2 * g + u) * P : (2 * g + u + 1) * P], node32[:, g, u, :], ident[:])
+            small32 = small_in[:].bitcast(F32)
+            nc.scalar.copy(
+                out=small32[0:96, 0:256].rearrange("p (j rep u) -> p j rep u", j=64, rep=2, u=2),
+                in_=pn[0:96, 0:256]
+                .rearrange("p (u c) -> p c u", u=2)[:, 0:64, :]
+                .unsqueeze(2)
+                .to_broadcast([96, 64, 2, 2]),
+            )
+            for g, lo, hi in ((0, 96, 128), (1, 0, 128)):
+                dst_out = small32[lo:hi, 256 * g : 256 * (g + 1)].rearrange(
+                    "p (m b rep kh u) -> p m b rep kh u", m=16, b=2, rep=2, kh=2, u=2
+                )
+                dst_in = pn[lo:hi, 256 * g : 256 * (g + 1)].rearrange(
+                    "p (u z b kh m) -> p z b m kh u", u=2, z=2, b=2, kh=2, m=16
+                )
+                for b in range(2):
+                    for rep in range(2):
+                        nc.scalar.copy(out=dst_out[:, :, b, rep, :, :], in_=dst_in[:, 0, b, :, :, :])
+            nc.vector.quantize_mx(out=small_codes[:].bitcast(FP8X4), scales=small_plane[:], in_=small_in[:])
+
+        def move(eng, dst, src):
+            if eng == "g":
+                nc.gpsimd.tensor_copy(out=dst, in_=src)
+            else:
+                nc.vector.tensor_copy(out=dst, in_=src)
+
+        def spread_dst(eng, g, lo, hi, m0, m1):
+            nm = m1 - m0
+            tcols = slice(P * m0, P * m1)
+            scols = slice(128 * g + 8 * m0, 128 * g + 8 * m1)
+            move(
+                eng,
+                t_codes[g][lo:hi, tcols].bitcast(I32).rearrange("p (mb i x) -> p mb i x", mb=2 * nm, i=16, x=4),
+                small_codes[lo:hi, scols]
+                .bitcast(I32)
+                .rearrange("p (mb x) -> p mb x", x=4)
+                .unsqueeze(2)
+                .to_broadcast([hi - lo, 2 * nm, 16, 4]),
+            )
+            move(
+                eng,
+                t_plane[g][lo:hi, tcols].bitcast(I32).rearrange("p (mb w) -> p mb w", mb=2 * nm),
+                small_plane[lo:hi, scols].bitcast(I32).unsqueeze(2).to_broadcast([hi - lo, 2 * nm, 16]),
+            )
+
+        def spread_pass0(eng, m0, m1):
+            nm = m1 - m0
+            tcols = slice(P * m0, P * m1)
+            move(
+                eng,
+                t_codes[0][0:96, tcols].bitcast(I32).rearrange("p (m r) -> p m r", m=nm),
+                small_codes[0:96, 0:128].bitcast(I32).unsqueeze(1).to_broadcast([96, nm, 128]),
+            )
+            move(
+                eng,
+                t_plane[0][0:96, tcols].bitcast(I32).rearrange("p (m w) -> p m w", m=nm),
+                small_plane[0:96, 0:128].bitcast(I32).unsqueeze(1).to_broadcast([96, nm, 32]),
+            )
+            spread_dst(eng, 0, 96, 128, m0, m1)
 
         edge32 = edge_sb[:].bitcast(F32).rearrange("r (x u) -> r u x", u=2)
-        for grp in range(4):
+
+        def edge_prep(grp, engs):
             g1 = stage.tile([P, 2048], BF16, align_bytes=64, tag="g1")
             g1_32 = g1[:].bitcast(F32)
             for pair in range(2):
@@ -121,70 +163,134 @@ def tile_edge_update_only_pa_kernel(tc, node_fts, edge_fts, Wt, out):
                             edge32[:, u, 64 * m : 64 * m + P],
                             ident[:],
                         )
-                nc.scalar.copy(
-                    out=g1_32[:, 512 * pair : 512 * (pair + 1)].rearrange("p (mm r u) -> p mm r u", mm=2, u=2),
-                    in_=pe_bank[:].rearrange("p (mm u r) -> p mm r u", mm=2, u=2),
+                bank_copy(
+                    engs[pair],
+                    g1_32[:, 512 * pair : 512 * (pair + 1)].rearrange("p (mm r u) -> p mm r u", mm=2, u=2),
+                    pe_bank[:].rearrange("p (mm u r) -> p mm r u", mm=2, u=2),
                 )
             cols = slice(512 * grp, 512 * (grp + 1))
             nc.vector.quantize_mx(out=t_codes[1][:, cols].bitcast(FP8X4), scales=t_plane[1][:, cols], in_=g1[:])
-        nc.vector.tensor_copy(
-            out=t_codes[1][0:64, :].bitcast(I32).rearrange("p (mb i x) -> p mb i x", mb=32, i=16, x=4),
-            in_=small_codes[0:64, 128:256]
-            .bitcast(I32)
-            .rearrange("p (mb x) -> p mb x", x=4)
-            .unsqueeze(2)
-            .to_broadcast([64, 32, 16, 4]),
-        )
-        nc.vector.tensor_copy(
-            out=t_plane[1][0:64, :].bitcast(I32).rearrange("p (mb w) -> p mb w", mb=32),
-            in_=small_plane[0:64, 128:256].bitcast(I32).unsqueeze(2).to_broadcast([64, 32, 16]),
-        )
 
         wt32 = wt_sb[:].bitcast(F32).rearrange("q c (s g w u) -> q c s g u w", s=2, g=2, w=P, u=2)
-        for cp in range(4):
-            for g in range(2):
-                gw = stage.tile([P, 2048], BF16, align_bytes=64, tag="gw")
-                gw32 = gw[:].bitcast(F32)
-                for half in range(2):
-                    c = 2 * cp + half
-                    pw = psum.tile([P, 512], F32, tag="bank")
-                    for s in range(2):
-                        for u in range(2):
-                            nc.tensor.transpose(
-                                pw[:, (2 * s + u) * P : (2 * s + u + 1) * P], wt32[:, c, s, g, u, :], ident[:]
-                            )
-                    nc.scalar.copy(
-                        out=gw32[:, 512 * half : 512 * (half + 1)].rearrange("p (q x) -> p q x", x=4),
-                        in_=pw[:].rearrange("p (x q) -> p q x", x=4),
-                    )
-                cols = slice(512 * cp, 512 * (cp + 1))
-                nc.vector.quantize_mx(out=w_codes[:, g, cols].bitcast(FP8X4), scales=w_plane[:, g, cols], in_=gw[:])
+        gws = {}
 
-        for m in range(TILES):
-            rows = slice(P * m, P * (m + 1))
-            for hh in range(2):
-                o = opool.tile([P, 1024], F32, tag="o")
-                for cc in range(2):
-                    cols = slice(1024 * hh + 512 * cc, 1024 * hh + 512 * (cc + 1))
-                    acc = psum.tile([P, 512], F32, tag="bank")
-                    for g in range(2):
-                        nc.tensor.matmul_mx(
-                            out=acc[:],
-                            lhsT=t_codes[g][:, rows].bitcast(FP8X4),
-                            lhsT_scale=t_plane[g][:, rows],
-                            rhs=w_codes[:, g, cols].bitcast(FP8X4),
-                            rhs_scale=w_plane[:, g, cols],
-                            start=(g == 0),
-                            stop=(g == 1),
+        def w_turn(c, engs):
+            half = c % 2
+            for g in range(2):
+                if half == 0:
+                    gws[g] = stage.tile([P, 2048], BF16, align_bytes=64, tag="gw", name="gw")
+                pw = psum.tile([P, 512], F32, tag="bank")
+                for s in range(2):
+                    for u in range(2):
+                        nc.tensor.transpose(
+                            pw[:, (2 * s + u) * P : (2 * s + u + 1) * P], wt32[:, c, s, g, u, :], ident[:]
                         )
-                    y = ypool.tile([P, 512], F32, tag="y")
-                    nc.scalar.copy(out=y[:], in_=acc[:])
-                    nc.vector.scalar_tensor_tensor(
-                        out=o[:, 512 * cc : 512 * (cc + 1)],
-                        in0=acc[:],
-                        scalar=0.1,
-                        in1=y[:],
-                        op0=mybir.AluOpType.mult,
-                        op1=mybir.AluOpType.max,
+                bank_copy(
+                    engs[g],
+                    gws[g][:].bitcast(F32)[:, 512 * half : 512 * (half + 1)].rearrange("p (q x) -> p q x", x=4),
+                    pw[:].rearrange("p (x q) -> p q x", x=4),
+                )
+
+        def w_quant(cp):
+            cols = slice(512 * cp, 512 * (cp + 1))
+            for g in range(2):
+                nc.vector.quantize_mx(
+                    out=w_codes[:, g, cols].bitcast(FP8X4), scales=w_plane[:, g, cols], in_=gws[g][:]
+                )
+
+        def sums(m, cp):
+            rows = slice(P * m, P * (m + 1))
+            cols = slice(512 * cp, 512 * (cp + 1))
+            acc = psum.tile([P, 512], F32, tag="bank")
+            for g in range(2):
+                nc.tensor.matmul_mx(
+                    out=acc[:],
+                    lhsT=t_codes[g][:, rows].bitcast(FP8X4),
+                    lhsT_scale=t_plane[g][:, rows],
+                    rhs=w_codes[:, g, cols].bitcast(FP8X4),
+                    rhs_scale=w_plane[:, g, cols],
+                    start=(g == 0),
+                    stop=(g == 1),
+                )
+            return acc
+
+        outs = {}
+        late = {}
+        count = [0]
+
+        def store(m, hh, o):
+            nc.sync.dma_start(out=out_view[:, m, 1024 * hh : 1024 * (hh + 1)], in_=o[:])
+
+        def tick():
+            count[0] = count[0] + 1
+            if count[0] in late:
+                store(late[count[0]][0], late[count[0]][1], late[count[0]][2])
+
+        def bank(m, cp):
+            hh = cp // 2
+            cc = cp % 2
+            half = slice(512 * cc, 512 * (cc + 1))
+            to_gpsimd = (m, hh) in GPSIMD_UNITS
+            if (m, hh) not in outs:
+                if to_gpsimd:
+                    outs[(m, hh)] = gpool.tile([P, 1024], F32, tag="og", name="og")
+                else:
+                    outs[(m, hh)] = opool.tile([P, 1024], F32, tag="o", name="o")
+            o = outs[(m, hh)]
+            acc = sums(m, cp)
+            if to_gpsimd:
+                bank_copy("sv"[cc], o[:, half], acc[:])
+                if cc == 1:
+                    ng = gpool.tile([P, 1024], F32, tag="ng")
+                    nc.gpsimd.tensor_scalar(
+                        out=ng[:], in0=o[:], scalar1=0.0, scalar2=-3.0e38,
+                        op0=mybir.AluOpType.min, op1=mybir.AluOpType.max,
                     )
-                nc.sync.dma_start(out=out_view[:, m, 1024 * hh : 1024 * (hh + 1)], in_=o[:])
+                    nc.gpsimd.tensor_scalar(
+                        out=ng[:], in0=ng[:], scalar1=-0.9, scalar2=0.0,
+                        op0=mybir.AluOpType.mult, op1=mybir.AluOpType.add,
+                    )
+                    nc.gpsimd.tensor_tensor(out=o[:], in0=o[:], in1=ng[:], op=mybir.AluOpType.add)
+                    late[count[0] + GPSIMD_LAG] = (m, hh, o)
+                    tick()
+                return
+            y = ypool.tile([P, 512], F32, tag="y")
+            nc.scalar.copy(out=y[:], in_=acc[:])
+            nc.vector.scalar_tensor_tensor(
+                out=o[:, half],
+                in0=acc[:],
+                scalar=0.1,
+                in1=y[:],
+                op0=mybir.AluOpType.mult,
+                op1=mybir.AluOpType.max,
+            )
+            if (m, hh) in ((0, 0), (TILES - 1, 1)):
+                nc.sync.dma_start(out=out_view[:, m, 512 * cp : 512 * (cp + 1)], in_=o[:, half])
+            elif cc == 1:
+                store(m, hh, o)
+                tick()
+
+        def unit(m, hh):
+            bank(m, 2 * hh)
+            bank(m, 2 * hh + 1)
+
+        GPSIMD_UNITS = ()
+        GPSIMD_LAG = 5
+        warm(4)
+        node_prep()
+        spread_pass0("v", 0, 4)
+        for grp in range(4):
+            edge_prep(grp, "ss")
+        spread_dst("v", 1, 0, 64, 0, 4)
+        for cp in range(4):
+            w_turn(2 * cp, "ss")
+            w_turn(2 * cp + 1, "sv")
+            w_quant(cp)
+        hold = const.tile([P, 16], U32)
+        move("g", hold[:].bitcast(I32), w_codes[:, 1, HID - 16 : HID].bitcast(I32))
+        for m in range(4, TILES, 2):
+            spread_pass0("g", m, m + 2)
+            spread_dst("g", 1, 0, 64, m, m + 2)
+        for m in range(TILES):
+            for hh in range(2):
+                unit(m, hh)

@@ -37,7 +37,7 @@ def tile_edge_update_only_pa_kernel(tc, node_fts, edge_fts, Wt, out):
         ctx.enter_context(tc.manual_schedule(engines={mybir.EngineType.Pool}))
 
         node_sb = const.tile([P, 1024], BF16)
-        edge_sb = const.tile([P, 17 * 256], BF16)
+        edge_sb = const.tile([P, 16 * 256], BF16)
         wt_sb = const.tile([P, 8, 2048], BF16)
         ident = const.tile([P, P], F32)
         warm_sb = const.tile([P, 512], BF16)
@@ -52,23 +52,23 @@ def tile_edge_update_only_pa_kernel(tc, node_fts, edge_fts, Wt, out):
         nc.vector.memset(warm_sb[:], 0.0)
         nc.vector.memset(node_sb[64:128, :], 0.0)
         nc.vector.memset(node_sb[0:64, 768:1024], 0.0)
-        nc.vector.memset(edge_sb[:, 0:256], 0.0)
+        nc.vector.memset(t_plane[1][:, 0:1024].bitcast(I32), 0)
         nc.vector.memset(small_plane[:].bitcast(I32), 0)
         def load_node():
             nc.sync.dma_start(out=node_sb[0:64, 0:384], in_=node_flat)
             nc.sync.dma_start(out=node_sb[0:64, 384:768], in_=node_flat)
 
         def load_edge(t0, t1):
-            nc.sync.dma_start(out=edge_sb[:, 256 + 256 * t0 : 256 + 256 * t1], in_=edge_view[:, 256 * t0 : 256 * t1])
+            nc.sync.dma_start(out=edge_sb[:, 256 * t0 : 256 * t1], in_=edge_view[:, 256 * t0 : 256 * t1])
 
         def load_w(c):
             nc.sync.dma_start(out=wt_sb[:, c, :], in_=wt_view[:, c, :])
 
         load_node()
         load_edge(0, 8)
-        load_edge(8, 16)
         for c in range(8):
             load_w(c)
+        load_edge(8, 16)
         make_identity(nc, ident[:])
 
         def warm(n):
@@ -98,14 +98,16 @@ def tile_edge_update_only_pa_kernel(tc, node_fts, edge_fts, Wt, out):
             )
             for g, lo, hi in ((0, 96, 128), (1, 0, 128)):
                 dst_out = small32[lo:hi, 256 * g : 256 * (g + 1)].rearrange(
-                    "p (m b rep kh u) -> p m b rep kh u", m=16, b=2, rep=2, kh=2, u=2
+                    ("p (j par b rep kh u) -> p par j b rep kh u", "p (par j b rep kh u) -> p par j b rep kh u")[g],
+                    par=2, j=8, b=2, rep=2, kh=2, u=2,
                 )
                 dst_in = pn[lo:hi, 256 * g : 256 * (g + 1)].rearrange(
-                    "p (u z b kh m) -> p z b m kh u", u=2, z=2, b=2, kh=2, m=16
+                    "p (u z b kh j par) -> p z b par j kh u", u=2, z=2, b=2, kh=2, j=8, par=2
                 )
                 for b in range(2):
                     for rep in range(2):
-                        nc.scalar.copy(out=dst_out[:, :, b, rep, :, :], in_=dst_in[:, 0, b, :, :, :])
+                        for par in range(2):
+                            nc.scalar.copy(out=dst_out[:, par, :, b, rep, :, :], in_=dst_in[:, 0, b, par, :, :, :])
             nc.vector.quantize_mx(out=small_codes[:].bitcast(FP8X4), scales=small_plane[:], in_=small_in[:])
 
         def move(eng, dst, src):
@@ -114,10 +116,9 @@ def tile_edge_update_only_pa_kernel(tc, node_fts, edge_fts, Wt, out):
             else:
                 nc.vector.tensor_copy(out=dst, in_=src)
 
-        def spread_dst(eng, g, lo, hi, m0, m1):
-            nm = m1 - m0
-            tcols = slice(P * m0, P * m1)
-            scols = slice(128 * g + 8 * m0, 128 * g + 8 * m1)
+        def spread_dst(eng, g, lo, hi, tcol0, scol0, nm):
+            tcols = slice(tcol0, tcol0 + P * nm)
+            scols = slice(scol0, scol0 + 8 * nm)
             move(
                 eng,
                 t_codes[g][lo:hi, tcols].bitcast(I32).rearrange("p (mb i x) -> p mb i x", mb=2 * nm, i=16, x=4),
@@ -146,30 +147,39 @@ def tile_edge_update_only_pa_kernel(tc, node_fts, edge_fts, Wt, out):
                 t_plane[0][0:96, tcols].bitcast(I32).rearrange("p (m w) -> p m w", m=nm),
                 small_plane[0:96, 0:128].bitcast(I32).unsqueeze(1).to_broadcast([96, nm, 32]),
             )
-            spread_dst(eng, 0, 96, 128, m0, m1)
+            spread_dst(eng, 0, 96, 128, P * m0, 8 * m0, nm)
+
+        def col1(m):
+            return 1024 * (1 - m % 2) + P * (m // 2)
+
+        def spread_pass1(eng, par, j0, j1):
+            spread_dst(eng, 1, 0, 64, col1(2 * j0 + par), 128 + 64 * par + 8 * j0, j1 - j0)
 
         edge32 = edge_sb[:].bitcast(F32).rearrange("r (x u) -> r u x", u=2)
 
-        def edge_prep(grp, engs):
+        def edge_prep(q, engs):
             g1 = stage.tile([P, 2048], BF16, align_bytes=64, tag="g1")
             g1_32 = g1[:].bitcast(F32)
             for pair in range(2):
                 pe_bank = psum.tile([P, 512], F32, tag="bank")
-                for mm in range(2):
-                    m = 4 * grp + 2 * pair + mm
+                for jj in range(2):
+                    j = 4 * q + 2 * pair + jj
                     for u in range(2):
                         nc.tensor.transpose(
-                            pe_bank[:, (2 * mm + u) * P : (2 * mm + u + 1) * P],
-                            edge32[:, u, 64 * m : 64 * m + P],
+                            pe_bank[:, (2 * jj + u) * P : (2 * jj + u + 1) * P],
+                            edge32[:, u, P * j : P * (j + 1)],
                             ident[:],
                         )
                 bank_copy(
                     engs[pair],
-                    g1_32[:, 512 * pair : 512 * (pair + 1)].rearrange("p (mm r u) -> p mm r u", mm=2, u=2),
-                    pe_bank[:].rearrange("p (mm u r) -> p mm r u", mm=2, u=2),
+                    g1_32[:, 512 * pair : 512 * (pair + 1)].rearrange("p (jj r u) -> p jj r u", jj=2, u=2),
+                    pe_bank[:].rearrange("p (jj u r) -> p jj r u", jj=2, u=2),
                 )
-            cols = slice(512 * grp, 512 * (grp + 1))
+            cols = slice(512 * q, 512 * (q + 1))
+            up = slice(1024 + 512 * q, 1024 + 512 * (q + 1))
             nc.vector.quantize_mx(out=t_codes[1][:, cols].bitcast(FP8X4), scales=t_plane[1][:, cols], in_=g1[:])
+            nc.sync.dma_start(out=t_codes[1][64:128, up].bitcast(I32), in_=t_codes[1][0:64, cols].bitcast(I32))
+            nc.sync.dma_start(out=t_plane[1][64:128, up].bitcast(I32), in_=t_plane[1][0:64, cols].bitcast(I32))
 
         wt32 = wt_sb[:].bitcast(F32).rearrange("q c (s g w u) -> q c s g u w", s=2, g=2, w=P, u=2)
         gws = {}
@@ -198,15 +208,15 @@ def tile_edge_update_only_pa_kernel(tc, node_fts, edge_fts, Wt, out):
                     out=w_codes[:, g, cols].bitcast(FP8X4), scales=w_plane[:, g, cols], in_=gws[g][:]
                 )
 
-        def sums(m, cp):
-            rows = slice(P * m, P * (m + 1))
-            cols = slice(512 * cp, 512 * (cp + 1))
-            acc = psum.tile([P, 512], F32, tag="bank")
+        def sums(m, c0, width):
+            rows = (slice(P * m, P * (m + 1)), slice(col1(m), col1(m) + P))
+            cols = slice(c0, c0 + width)
+            acc = psum.tile([P, width], F32, tag="bank")
             for g in range(2):
                 nc.tensor.matmul_mx(
                     out=acc[:],
-                    lhsT=t_codes[g][:, rows].bitcast(FP8X4),
-                    lhsT_scale=t_plane[g][:, rows],
+                    lhsT=t_codes[g][:, rows[g]].bitcast(FP8X4),
+                    lhsT_scale=t_plane[g][:, rows[g]],
                     rhs=w_codes[:, g, cols].bitcast(FP8X4),
                     rhs_scale=w_plane[:, g, cols],
                     start=(g == 0),
@@ -237,7 +247,7 @@ def tile_edge_update_only_pa_kernel(tc, node_fts, edge_fts, Wt, out):
                 else:
                     outs[(m, hh)] = opool.tile([P, 1024], F32, tag="o", name="o")
             o = outs[(m, hh)]
-            acc = sums(m, cp)
+            acc = sums(m, 512 * cp, 512)
             if to_gpsimd:
                 bank_copy("sv"[cc], o[:, half], acc[:])
                 if cc == 1:
@@ -264,11 +274,21 @@ def tile_edge_update_only_pa_kernel(tc, node_fts, edge_fts, Wt, out):
                 op0=mybir.AluOpType.mult,
                 op1=mybir.AluOpType.max,
             )
-            if (m, hh) in ((0, 0), (TILES - 1, 1)):
+            if (m, hh) == (0, 0):
                 nc.sync.dma_start(out=out_view[:, m, 512 * cp : 512 * (cp + 1)], in_=o[:, half])
             elif cc == 1:
                 store(m, hh, o)
                 tick()
+
+        def narrow(m, c0, width):
+            acc = sums(m, c0, width)
+            y = ypool.tile([P, width], F32, tag="y")
+            o = opool.tile([P, width], F32, tag="o")
+            nc.scalar.copy(out=y[:], in_=acc[:])
+            nc.vector.scalar_tensor_tensor(
+                out=o[:], in0=acc[:], scalar=0.1, in1=y[:], op0=mybir.AluOpType.mult, op1=mybir.AluOpType.max
+            )
+            nc.sync.dma_start(out=out_view[:, m, c0 : c0 + width], in_=o[:])
 
         def unit(m, hh):
             bank(m, 2 * hh)
@@ -279,18 +299,25 @@ def tile_edge_update_only_pa_kernel(tc, node_fts, edge_fts, Wt, out):
         warm(4)
         node_prep()
         spread_pass0("v", 0, 4)
-        for grp in range(4):
-            edge_prep(grp, "ss")
-        spread_dst("v", 1, 0, 64, 0, 4)
+        edge_prep(0, "ss")
+        spread_pass1("v", 0, 0, 2)
         for cp in range(4):
             w_turn(2 * cp, "ss")
-            w_turn(2 * cp + 1, "sv")
+            w_turn(2 * cp + 1, "sv" if cp < 3 else "ss")
             w_quant(cp)
+        spread_pass1("v", 1, 0, 2)
+        edge_prep(1, "ss")
         hold = const.tile([P, 16], U32)
         move("g", hold[:].bitcast(I32), w_codes[:, 1, HID - 16 : HID].bitcast(I32))
-        for m in range(4, TILES, 2):
-            spread_pass0("g", m, m + 2)
-            spread_dst("g", 1, 0, 64, m, m + 2)
-        for m in range(TILES):
+        for k in range(1, 4):
+            spread_pass0("g", 4 * k, 4 * k + 2)
+            spread_pass1("g", 0, 2 * k, 2 * k + 2)
+            spread_pass1("g", 1, 2 * k, 2 * k + 2)
+            spread_pass0("g", 4 * k + 2, 4 * k + 4)
+        for m in range(TILES - 1):
             for hh in range(2):
                 unit(m, hh)
+        unit(TILES - 1, 0)
+        narrow(TILES - 1, 1024, 512)
+        narrow(TILES - 1, 1536, 256)
+        narrow(TILES - 1, 1792, 256)

@@ -306,15 +306,24 @@ def tile_edge_update_only_pa_kernel(tc, node_fts, edge_fts, Wt, out):
             w_turn(2 * cp + 1, "sv" if cp < 3 else "ss")
             w_quant(cp)
         spread_pass1("v", 1, 0, 2)
-        edge_prep(1, "ss")
-        hold = const.tile([P, 16], U32)
-        move("g", hold[:].bitcast(I32), w_codes[:, 1, HID - 16 : HID].bitcast(I32))
-        for k in range(1, 4):
+
+        def spread_four(k):
             spread_pass0("g", 4 * k, 4 * k + 2)
             spread_pass1("g", 0, 2 * k, 2 * k + 2)
             spread_pass1("g", 1, 2 * k, 2 * k + 2)
             spread_pass0("g", 4 * k + 2, 4 * k + 4)
-        for m in range(TILES - 1):
+
+        hold = const.tile([P, 32], U32)
+        move("g", hold[:, 0:16].bitcast(I32), w_codes[:, 1, HID - 16 : HID].bitcast(I32))
+        spread_four(1)
+        for m in range(4):
+            for hh in range(2):
+                unit(m, hh)
+        edge_prep(1, "ss")
+        move("g", hold[:, 16:32].bitcast(I32), t_codes[1][:, 1024 - 16 : 1024].bitcast(I32))
+        spread_four(2)
+        spread_four(3)
+        for m in range(4, TILES - 1):
             for hh in range(2):
                 unit(m, hh)
         unit(TILES - 1, 0)

@@ -31,7 +31,7 @@ def tile_edge_update_only_pa_kernel(tc, node_fts, edge_fts, Wt, out):
         const = ctx.enter_context(tc.tile_pool(name="const", bufs=1))
         stage = ctx.enter_context(tc.tile_pool(name="stage", bufs=4))
         ypool = ctx.enter_context(tc.tile_pool(name="ypool", bufs=4))
-        opool = ctx.enter_context(tc.tile_pool(name="opool", bufs=6))
+        opool = ctx.enter_context(tc.tile_pool(name="opool", bufs=5))
         gpool = ctx.enter_context(tc.tile_pool(name="gpool", bufs=2))
         psum = ctx.enter_context(tc.psum_pool(name="psum", bufs=8))
         ctx.enter_context(tc.manual_schedule(engines={mybir.EngineType.Pool}))
@@ -237,48 +237,28 @@ def tile_edge_update_only_pa_kernel(tc, node_fts, edge_fts, Wt, out):
                 store(late[count[0]][0], late[count[0]][1], late[count[0]][2])
 
         def bank(m, cp):
-            hh = cp // 2
-            cc = cp % 2
-            half = slice(512 * cc, 512 * (cc + 1))
-            to_gpsimd = (m, hh) in GPSIMD_UNITS
-            if (m, hh) not in outs:
-                if to_gpsimd:
-                    outs[(m, hh)] = gpool.tile([P, 1024], F32, tag="og", name="og")
-                else:
-                    outs[(m, hh)] = opool.tile([P, 1024], F32, tag="o", name="o")
-            o = outs[(m, hh)]
+            whole = 0 < m < TILES - 1
+            width = 2048 if whole else 1024
+            key = (m, 0) if whole else (m, cp // 2)
+            if key not in outs:
+                outs[key] = opool.tile([P, width], F32, tag="o", name="o")
+            o = outs[key]
+            at = 512 * cp % width
             acc = sums(m, 512 * cp, 512)
-            if to_gpsimd:
-                bank_copy("sv"[cc], o[:, half], acc[:])
-                if cc == 1:
-                    ng = gpool.tile([P, 1024], F32, tag="ng")
-                    nc.gpsimd.tensor_scalar(
-                        out=ng[:], in0=o[:], scalar1=0.0, scalar2=-3.0e38,
-                        op0=mybir.AluOpType.min, op1=mybir.AluOpType.max,
-                    )
-                    nc.gpsimd.tensor_scalar(
-                        out=ng[:], in0=ng[:], scalar1=-0.9, scalar2=0.0,
-                        op0=mybir.AluOpType.mult, op1=mybir.AluOpType.add,
-                    )
-                    nc.gpsimd.tensor_tensor(out=o[:], in0=o[:], in1=ng[:], op=mybir.AluOpType.add)
-                    late[count[0] + GPSIMD_LAG] = (m, hh, o)
-                    tick()
-                return
             y = ypool.tile([P, 512], F32, tag="y")
             nc.scalar.copy(out=y[:], in_=acc[:])
             nc.vector.scalar_tensor_tensor(
-                out=o[:, half],
+                out=o[:, at : at + 512],
                 in0=acc[:],
                 scalar=0.1,
                 in1=y[:],
                 op0=mybir.AluOpType.mult,
                 op1=mybir.AluOpType.max,
             )
-            if (m, hh) == (0, 0):
-                nc.sync.dma_start(out=out_view[:, m, 512 * cp : 512 * (cp + 1)], in_=o[:, half])
-            elif cc == 1:
-                store(m, hh, o)
-                tick()
+            if m == 0 and cp < 2:
+                nc.sync.dma_start(out=out_view[:, m, 512 * cp : 512 * (cp + 1)], in_=o[:, at : at + 512])
+            elif at + 512 == width:
+                nc.sync.dma_start(out=out_view[:, m, 512 * (cp + 1) - width : 512 * (cp + 1)], in_=o[:])
 
         def narrow(m, c0, width):
             acc = sums(m, c0, width)

@@ -23,27 +23,26 @@ def tile_edge_update_only_pa_kernel(tc, node_fts, edge_fts, Wt, out):
     node_flat = node_fts.flatten_outer_dims()
     edge_flat = edge_fts.flatten_outer_dims()
     out_flat = out.flatten_outer_dims()
-    edge_view = edge_flat.rearrange("(r m) c -> r (m c)", m=TILES)
+    edge_view = edge_flat.rearrange("(b r s) c -> r b (s c)", b=2, s=8)
     wt_view = Wt.rearrange("(c q s) k -> q c (s k)", q=P, s=2)
-    out_view = out_flat.rearrange("(r m) h -> r m h", m=TILES)
+    out_view = out_flat.rearrange("(b r s) h -> r b s h", b=2, s=8)
 
     with ExitStack() as ctx:
         const = ctx.enter_context(tc.tile_pool(name="const", bufs=1))
         stage = ctx.enter_context(tc.tile_pool(name="stage", bufs=4))
         ypool = ctx.enter_context(tc.tile_pool(name="ypool", bufs=4))
-        opool = ctx.enter_context(tc.tile_pool(name="opool", bufs=5))
-        gpool = ctx.enter_context(tc.tile_pool(name="gpool", bufs=2))
+        opool = ctx.enter_context(tc.tile_pool(name="opool", bufs=10))
         psum = ctx.enter_context(tc.psum_pool(name="psum", bufs=8))
-        ctx.enter_context(tc.manual_schedule(engines={mybir.EngineType.Pool}))
+        ctx.enter_context(tc.manual_schedule())
 
         node_sb = const.tile([P, 1024], BF16)
         edge_sb = const.tile([P, 16 * 256], BF16)
         wt_sb = const.tile([P, 8, 2048], BF16)
         ident = const.tile([P, P], F32)
         warm_sb = const.tile([P, 512], BF16)
-        small_in = const.tile([P, 1024], BF16, align_bytes=64)
-        small_codes = const.tile([P, 256], U32, align_bytes=64)
-        small_plane = const.tile([P, 256], U8, align_bytes=64)
+        small_in = const.tile([P, 1280], BF16, align_bytes=64)
+        small_codes = const.tile([P, 320], U32, align_bytes=64)
+        small_plane = const.tile([P, 320], U8, align_bytes=64)
         w_codes = const.tile([P, 2, HID], U32, align_bytes=64)
         w_plane = const.tile([P, 2, HID], U8, align_bytes=64)
         t_codes = [const.tile([P, ROWS], U32, align_bytes=64, name="t_codes%d" % g) for g in range(2)]
@@ -54,21 +53,24 @@ def tile_edge_update_only_pa_kernel(tc, node_fts, edge_fts, Wt, out):
         nc.vector.memset(node_sb[0:64, 768:1024], 0.0)
         nc.vector.memset(t_plane[1][:, 0:1024].bitcast(I32), 0)
         nc.vector.memset(small_plane[:].bitcast(I32), 0)
+        nc.gpsimd.memset(small_in[96:128, 0:1024].bitcast(F32), 0.0)
         def load_node():
             nc.sync.dma_start(out=node_sb[0:64, 0:384], in_=node_flat)
             nc.sync.dma_start(out=node_sb[0:64, 384:768], in_=node_flat)
 
         def load_edge(t0, t1):
-            nc.sync.dma_start(out=edge_sb[:, 256 * t0 : 256 * t1], in_=edge_view[:, 256 * t0 : 256 * t1])
+            b, s0 = divmod(t0, 8)
+            nc.sync.dma_start(
+                out=edge_sb[:, 256 * t0 : 256 * t1], in_=edge_view[:, b, 256 * s0 : 256 * (s0 + t1 - t0)]
+            )
 
         def load_w(c):
             nc.sync.dma_start(out=wt_sb[:, c, :], in_=wt_view[:, c, :])
 
         load_node()
         load_edge(0, 8)
-        for c in range(8):
+        for c in range(6):
             load_w(c)
-        load_edge(8, 16)
         make_identity(nc, ident[:])
 
         def warm(n):
@@ -90,25 +92,25 @@ def tile_edge_update_only_pa_kernel(tc, node_fts, edge_fts, Wt, out):
                     nc.tensor.transpose(pn[:, (2 * g + u) * P : (2 * g + u + 1) * P], node32[:, g, u, :], ident[:])
             small32 = small_in[:].bitcast(F32)
             nc.scalar.copy(
-                out=small32[0:96, 0:256].rearrange("p (j rep u) -> p j rep u", j=64, rep=2, u=2),
+                out=small32[0:96, 0:512].rearrange("p (c rep u) -> p c rep u", c=64, rep=4, u=2),
                 in_=pn[0:96, 0:256]
                 .rearrange("p (u c) -> p c u", u=2)[:, 0:64, :]
                 .unsqueeze(2)
-                .to_broadcast([96, 64, 2, 2]),
+                .to_broadcast([96, 64, 4, 2]),
             )
             for g, lo, hi in ((0, 96, 128), (1, 0, 128)):
-                dst_out = small32[lo:hi, 256 * g : 256 * (g + 1)].rearrange(
-                    ("p (j par b rep kh u) -> p par j b rep kh u", "p (par j b rep kh u) -> p par j b rep kh u")[g],
-                    par=2, j=8, b=2, rep=2, kh=2, u=2,
-                )
-                dst_in = pn[lo:hi, 256 * g : 256 * (g + 1)].rearrange(
-                    "p (u z b kh j par) -> p z b par j kh u", u=2, z=2, b=2, kh=2, j=8, par=2
+                dst_in = pn[lo:hi, 256 * g : 256 * (g + 1)].rearrange("p (u z b kq s) -> p z b s kq u", u=2, z=2, b=2, kq=4, s=8)
+                dst_out = small32[lo:hi, 512 * g : 512 * g + 128].rearrange(
+                    "p (b s kq u) -> p b s kq u", b=2, s=8, kq=4, u=2
                 )
                 for b in range(2):
-                    for rep in range(2):
-                        for par in range(2):
-                            nc.scalar.copy(out=dst_out[:, par, :, b, rep, :, :], in_=dst_in[:, 0, b, par, :, :, :])
-            nc.vector.quantize_mx(out=small_codes[:].bitcast(FP8X4), scales=small_plane[:], in_=small_in[:])
+                    nc.scalar.copy(out=dst_out[:, b, :, :, :], in_=dst_in[:, 0, b, :, :, :])
+            for c0, c1 in ((0, 256), (256, 320)):
+                nc.vector.quantize_mx(
+                    out=small_codes[:, c0:c1].bitcast(FP8X4),
+                    scales=small_plane[:, c0:c1],
+                    in_=small_in[:, 4 * c0 : 4 * c1],
+                )
 
         def move(eng, dst, src):
             if eng == "g":
@@ -116,44 +118,51 @@ def tile_edge_update_only_pa_kernel(tc, node_fts, edge_fts, Wt, out):
             else:
                 nc.vector.tensor_copy(out=dst, in_=src)
 
-        def spread_dst(eng, g, lo, hi, tcol0, scol0, nm):
+        def spread_dst(eng, g, lo, hi, tcol0, m0, nm, step):
             tcols = slice(tcol0, tcol0 + P * nm)
-            scols = slice(scol0, scol0 + 8 * nm)
+            at = m0 % step
+            scols = slice(256 * g + 4 * (m0 - at), 256 * g + 4 * (m0 - at + step * nm))
             move(
                 eng,
-                t_codes[g][lo:hi, tcols].bitcast(I32).rearrange("p (mb i x) -> p mb i x", mb=2 * nm, i=16, x=4),
+                t_codes[g][lo:hi, tcols].bitcast(I32).rearrange("p (m i x) -> p m i x", m=nm, i=32, x=4),
                 small_codes[lo:hi, scols]
                 .bitcast(I32)
-                .rearrange("p (mb x) -> p mb x", x=4)
+                .rearrange("p (m z x) -> p m z x", z=step, x=4)[:, :, at, :]
                 .unsqueeze(2)
-                .to_broadcast([hi - lo, 2 * nm, 16, 4]),
+                .to_broadcast([hi - lo, nm, 32, 4]),
             )
             move(
                 eng,
-                t_plane[g][lo:hi, tcols].bitcast(I32).rearrange("p (mb w) -> p mb w", mb=2 * nm),
-                small_plane[lo:hi, scols].bitcast(I32).unsqueeze(2).to_broadcast([hi - lo, 2 * nm, 16]),
+                t_plane[g][lo:hi, tcols].bitcast(I32).rearrange("p (m w) -> p m w", m=nm),
+                small_plane[lo:hi, scols]
+                .bitcast(I32)
+                .rearrange("p (m z) -> p m z", z=step)[:, :, at]
+                .unsqueeze(2)
+                .to_broadcast([hi - lo, nm, 32]),
             )
 
         def spread_pass0(eng, m0, m1):
             nm = m1 - m0
+            b = m0 // 8
             tcols = slice(P * m0, P * m1)
+            scols = slice(P * b, P * (b + 1))
             move(
                 eng,
                 t_codes[0][0:96, tcols].bitcast(I32).rearrange("p (m r) -> p m r", m=nm),
-                small_codes[0:96, 0:128].bitcast(I32).unsqueeze(1).to_broadcast([96, nm, 128]),
+                small_codes[0:96, scols].bitcast(I32).unsqueeze(1).to_broadcast([96, nm, 128]),
             )
             move(
                 eng,
                 t_plane[0][0:96, tcols].bitcast(I32).rearrange("p (m w) -> p m w", m=nm),
-                small_plane[0:96, 0:128].bitcast(I32).unsqueeze(1).to_broadcast([96, nm, 32]),
+                small_plane[0:96, scols].bitcast(I32).unsqueeze(1).to_broadcast([96, nm, 32]),
             )
-            spread_dst(eng, 0, 96, 128, P * m0, 8 * m0, nm)
+            spread_dst(eng, 0, 96, 128, P * m0, m0, nm, 1)
 
         def col1(m):
             return 1024 * (1 - m % 2) + P * (m // 2)
 
         def spread_pass1(eng, par, j0, j1):
-            spread_dst(eng, 1, 0, 64, col1(2 * j0 + par), 128 + 64 * par + 8 * j0, j1 - j0)
+            spread_dst(eng, 1, 0, 64, col1(2 * j0 + par), 2 * j0 + par, j1 - j0, 2)
 
         edge32 = edge_sb[:].bitcast(F32).rearrange("r (x u) -> r u x", u=2)
 
@@ -225,19 +234,9 @@ def tile_edge_update_only_pa_kernel(tc, node_fts, edge_fts, Wt, out):
             return acc
 
         outs = {}
-        late = {}
-        count = [0]
-
-        def store(m, hh, o):
-            nc.sync.dma_start(out=out_view[:, m, 1024 * hh : 1024 * (hh + 1)], in_=o[:])
-
-        def tick():
-            count[0] = count[0] + 1
-            if count[0] in late:
-                store(late[count[0]][0], late[count[0]][1], late[count[0]][2])
 
         def bank(m, cp):
-            whole = 0 < m < TILES - 1
+            whole = False
             width = 2048 if whole else 1024
             key = (m, 0) if whole else (m, cp // 2)
             if key not in outs:
@@ -255,10 +254,9 @@ def tile_edge_update_only_pa_kernel(tc, node_fts, edge_fts, Wt, out):
                 op0=mybir.AluOpType.mult,
                 op1=mybir.AluOpType.max,
             )
-            if m == 0 and cp < 2:
-                nc.sync.dma_start(out=out_view[:, m, 512 * cp : 512 * (cp + 1)], in_=o[:, at : at + 512])
-            elif at + 512 == width:
-                nc.sync.dma_start(out=out_view[:, m, 512 * (cp + 1) - width : 512 * (cp + 1)], in_=o[:])
+
+        def store_half(m, h):
+            nc.sync.dma_start(out=out_view[:, m // 8, m % 8, 1024 * h : 1024 * (h + 1)], in_=outs[(m, h)][:])
 
         def narrow(m, c0, width):
             acc = sums(m, c0, width)
@@ -268,24 +266,11 @@ def tile_edge_update_only_pa_kernel(tc, node_fts, edge_fts, Wt, out):
             nc.vector.scalar_tensor_tensor(
                 out=o[:], in0=acc[:], scalar=0.1, in1=y[:], op0=mybir.AluOpType.mult, op1=mybir.AluOpType.max
             )
-            nc.sync.dma_start(out=out_view[:, m, c0 : c0 + width], in_=o[:])
+            nc.sync.dma_start(out=out_view[:, m // 8, m % 8, c0 : c0 + width], in_=o[:])
 
         def unit(m, hh):
             bank(m, 2 * hh)
             bank(m, 2 * hh + 1)
-
-        GPSIMD_UNITS = ()
-        GPSIMD_LAG = 5
-        warm(4)
-        node_prep()
-        spread_pass0("v", 0, 4)
-        edge_prep(0, "ss")
-        spread_pass1("v", 0, 0, 2)
-        for cp in range(4):
-            w_turn(2 * cp, "ss")
-            w_turn(2 * cp + 1, "sv" if cp < 3 else "ss")
-            w_quant(cp)
-        spread_pass1("v", 1, 0, 2)
 
         def spread_four(k):
             spread_pass0("g", 4 * k, 4 * k + 2)
@@ -294,19 +279,53 @@ def tile_edge_update_only_pa_kernel(tc, node_fts, edge_fts, Wt, out):
             spread_pass0("g", 4 * k + 2, 4 * k + 4)
 
         hold = const.tile([P, 32], U32)
+        warm(4)
+        node_prep()
+        spread_pass0("v", 0, 4)
+        edge_prep(0, "ss")
+        for c in (6, 7):
+            load_w(c)
+        load_edge(8, 16)
+        def half(m, h):
+            bank(m, 2 * h)
+            bank(m, 2 * h + 1)
+            store_half(m, h)
+        def spread_four(k):
+            spread_pass0("g", 4 * k, 4 * k + 2)
+            spread_pass1("g", 0, 2 * k, 2 * k + 2)
+            spread_pass1("g", 1, 2 * k, 2 * k + 2)
+            spread_pass0("g", 4 * k + 2, 4 * k + 4)
+        VC = ("ss", "sv", "ss", "sv", "ss", "ss", "ss", "ss")
+        def W(c):
+            w_turn(c, VC[c])
+            if c % 2 == 1:
+                w_quant(c // 2)
+        W(0)
+        W(1)
+        W(2)
+        W(3)
+        spread_pass1("v", 0, 0, 2)
+        W(4)
+        spread_pass1("v", 1, 0, 2)
+        W(5)
+        half(0, 0)
+        half(1, 0)
+        W(6)
+        W(7)
+        half(2, 0)
+        half(3, 0)
+        for m in range(4):
+            half(m, 1)
         move("g", hold[:, 0:16].bitcast(I32), w_codes[:, 1, HID - 16 : HID].bitcast(I32))
         spread_four(1)
-        for m in range(4):
-            for hh in range(2):
-                unit(m, hh)
         edge_prep(1, "ss")
         move("g", hold[:, 16:32].bitcast(I32), t_codes[1][:, 1024 - 16 : 1024].bitcast(I32))
         spread_four(2)
         spread_four(3)
-        for m in range(4, TILES - 1):
-            for hh in range(2):
-                unit(m, hh)
-        unit(TILES - 1, 0)
+        for m in range(4, 15):
+            for h in range(2):
+                half(m, h)
+        half(15, 0)
         narrow(TILES - 1, 1024, 512)
         narrow(TILES - 1, 1536, 256)
         narrow(TILES - 1, 1792, 256)

@@ -15,6 +15,7 @@ ROWS = 2048
 HID = 2048
 D_IN = 1024
 TILES = 16
+SLOTS = 8
 FLOPS = 2 * ROWS * D_IN * HID
 
 
@@ -31,7 +32,7 @@ def tile_edge_update_only_pa_kernel(tc, node_fts, edge_fts, Wt, out):
         const = ctx.enter_context(tc.tile_pool(name="const", bufs=1))
         stage = ctx.enter_context(tc.tile_pool(name="stage", bufs=4))
         ypool = ctx.enter_context(tc.tile_pool(name="ypool", bufs=4))
-        opool = ctx.enter_context(tc.tile_pool(name="opool", bufs=10))
+        opool = ctx.enter_context(tc.tile_pool(name="opool", bufs=8))
         psum = ctx.enter_context(tc.psum_pool(name="psum", bufs=8))
         ctx.enter_context(tc.manual_schedule())
 
@@ -45,8 +46,8 @@ def tile_edge_update_only_pa_kernel(tc, node_fts, edge_fts, Wt, out):
         small_plane = const.tile([P, 320], U8, align_bytes=64)
         w_codes = const.tile([P, 2, HID], U32, align_bytes=64)
         w_plane = const.tile([P, 2, HID], U8, align_bytes=64)
-        t_codes = [const.tile([P, ROWS], U32, align_bytes=64, name="t_codes%d" % g) for g in range(2)]
-        t_plane = [const.tile([P, ROWS], U8, align_bytes=64, name="t_plane%d" % g) for g in range(2)]
+        t_codes = [const.tile([P, (P * SLOTS, ROWS)[g]], U32, align_bytes=64, name="t_codes%d" % g) for g in range(2)]
+        t_plane = [const.tile([P, (P * SLOTS, ROWS)[g]], U8, align_bytes=64, name="t_plane%d" % g) for g in range(2)]
 
         nc.vector.memset(warm_sb[:], 0.0)
         nc.vector.memset(node_sb[64:128, :], 0.0)
@@ -68,7 +69,7 @@ def tile_edge_update_only_pa_kernel(tc, node_fts, edge_fts, Wt, out):
             nc.sync.dma_start(out=wt_sb[:, c, :], in_=wt_view[:, c, :])
 
         load_node()
-        load_edge(0, 8)
+        load_edge(0, 4)
         for c in range(6):
             load_w(c)
         make_identity(nc, ident[:])
@@ -141,51 +142,56 @@ def tile_edge_update_only_pa_kernel(tc, node_fts, edge_fts, Wt, out):
                 .to_broadcast([hi - lo, nm, 32]),
             )
 
-        def spread_pass0(eng, m0, m1):
-            nm = m1 - m0
-            b = m0 // 8
-            tcols = slice(P * m0, P * m1)
+        def spread_src(eng, b):
+            tcols = slice(4 * P * b, 4 * P * (b + 1))
             scols = slice(P * b, P * (b + 1))
             move(
                 eng,
-                t_codes[0][0:96, tcols].bitcast(I32).rearrange("p (m r) -> p m r", m=nm),
-                small_codes[0:96, scols].bitcast(I32).unsqueeze(1).to_broadcast([96, nm, 128]),
+                t_codes[0][0:96, tcols].bitcast(I32).rearrange("p (m r) -> p m r", m=4),
+                small_codes[0:96, scols].bitcast(I32).unsqueeze(1).to_broadcast([96, 4, 128]),
             )
             move(
                 eng,
-                t_plane[0][0:96, tcols].bitcast(I32).rearrange("p (m w) -> p m w", m=nm),
-                small_plane[0:96, scols].bitcast(I32).unsqueeze(1).to_broadcast([96, nm, 32]),
+                t_plane[0][0:96, tcols].bitcast(I32).rearrange("p (m w) -> p m w", m=4),
+                small_plane[0:96, scols].bitcast(I32).unsqueeze(1).to_broadcast([96, 4, 32]),
             )
-            spread_dst(eng, 0, 96, 128, P * m0, m0, nm, 1)
+
+        def col0(m):
+            return P * (4 * (m // 8) + m % 4)
 
         def col1(m):
             return 1024 * (1 - m % 2) + P * (m // 2)
+
+        def spread_pass0(eng, m0, nm):
+            spread_dst(eng, 0, 96, 128, col0(m0), m0, nm, 1)
+
+        def spread_tile(m):
+            spread_pass1("g", m % 2, m // 2, m // 2 + 1)
+            spread_pass0("g", m, 1)
 
         def spread_pass1(eng, par, j0, j1):
             spread_dst(eng, 1, 0, 64, col1(2 * j0 + par), 2 * j0 + par, j1 - j0, 2)
 
         edge32 = edge_sb[:].bitcast(F32).rearrange("r (x u) -> r u x", u=2)
 
-        def edge_prep(q, engs):
-            g1 = stage.tile([P, 2048], BF16, align_bytes=64, tag="g1")
-            g1_32 = g1[:].bitcast(F32)
-            for pair in range(2):
-                pe_bank = psum.tile([P, 512], F32, tag="bank")
-                for jj in range(2):
-                    j = 4 * q + 2 * pair + jj
-                    for u in range(2):
-                        nc.tensor.transpose(
-                            pe_bank[:, (2 * jj + u) * P : (2 * jj + u + 1) * P],
-                            edge32[:, u, P * j : P * (j + 1)],
-                            ident[:],
-                        )
-                bank_copy(
-                    engs[pair],
-                    g1_32[:, 512 * pair : 512 * (pair + 1)].rearrange("p (jj r u) -> p jj r u", jj=2, u=2),
-                    pe_bank[:].rearrange("p (jj u r) -> p jj r u", jj=2, u=2),
-                )
-            cols = slice(512 * q, 512 * (q + 1))
-            up = slice(1024 + 512 * q, 1024 + 512 * (q + 1))
+        def edge_prep(q, eng):
+            g1 = stage.tile([P, 1024], BF16, align_bytes=64, tag="g1")
+            pe_bank = psum.tile([P, 512], F32, tag="bank")
+            for jj in range(2):
+                j = 2 * q + jj
+                for u in range(2):
+                    nc.tensor.transpose(
+                        pe_bank[:, (2 * jj + u) * P : (2 * jj + u + 1) * P],
+                        edge32[:, u, P * j : P * (j + 1)],
+                        ident[:],
+                    )
+            bank_copy(
+                eng,
+                g1[:].bitcast(F32).rearrange("p (jj r u) -> p jj r u", jj=2, u=2),
+                pe_bank[:].rearrange("p (jj u r) -> p jj r u", jj=2, u=2),
+            )
+            cols = slice(256 * q, 256 * (q + 1))
+            up = slice(1024 + 256 * q, 1024 + 256 * (q + 1))
             nc.vector.quantize_mx(out=t_codes[1][:, cols].bitcast(FP8X4), scales=t_plane[1][:, cols], in_=g1[:])
             nc.sync.dma_start(out=t_codes[1][64:128, up].bitcast(I32), in_=t_codes[1][0:64, cols].bitcast(I32))
             nc.sync.dma_start(out=t_plane[1][64:128, up].bitcast(I32), in_=t_plane[1][0:64, cols].bitcast(I32))
@@ -218,7 +224,7 @@ def tile_edge_update_only_pa_kernel(tc, node_fts, edge_fts, Wt, out):
                 )
 
         def sums(m, c0, width):
-            rows = (slice(P * m, P * (m + 1)), slice(col1(m), col1(m) + P))
+            rows = (slice(col0(m), col0(m) + P), slice(col1(m), col1(m) + P))
             cols = slice(c0, c0 + width)
             acc = psum.tile([P, width], F32, tag="bank")
             for g in range(2):
@@ -279,52 +285,62 @@ def tile_edge_update_only_pa_kernel(tc, node_fts, edge_fts, Wt, out):
             spread_pass0("g", 4 * k + 2, 4 * k + 4)
 
         hold = const.tile([P, 32], U32)
-        warm(4)
-        node_prep()
-        spread_pass0("v", 0, 4)
-        edge_prep(0, "ss")
-        for c in (6, 7):
-            load_w(c)
-        load_edge(8, 16)
+
         def half(m, h):
             bank(m, 2 * h)
             bank(m, 2 * h + 1)
             store_half(m, h)
-        def spread_four(k):
-            spread_pass0("g", 4 * k, 4 * k + 2)
-            spread_pass1("g", 0, 2 * k, 2 * k + 2)
-            spread_pass1("g", 1, 2 * k, 2 * k + 2)
-            spread_pass0("g", 4 * k + 2, 4 * k + 4)
-        VC = ("ss", "sv", "ss", "sv", "ss", "ss", "ss", "ss")
-        def W(c):
-            w_turn(c, VC[c])
+
+        def W(c, engs="ss"):
+            w_turn(c, engs)
             if c % 2 == 1:
                 w_quant(c // 2)
-        W(0)
-        W(1)
-        W(2)
-        W(3)
+
+        def wait_g(n, src):
+            move("g", hold[:, 16 * n : 16 * n + 16].bitcast(I32), src.bitcast(I32))
+
+        warm(4)
+        node_prep()
+        spread_src("v", 0)
+        spread_pass0("v", 0, 4)
+        edge_prep(0, "s")
+        load_w(6)
+        load_w(7)
+        load_edge(4, 8)
+        load_edge(8, 12)
+        load_edge(12, 16)
+        W(0, "ss")
+        W(1, "sv")
+        W(2, "ss")
+        W(3, "sv")
         spread_pass1("v", 0, 0, 2)
-        W(4)
+        W(4, "ss")
         spread_pass1("v", 1, 0, 2)
-        W(5)
+        W(5, "ss")
         half(0, 0)
         half(1, 0)
-        W(6)
-        W(7)
+        W(6, "ss")
+        W(7, "ss")
+        edge_prep(1, "s")
         half(2, 0)
         half(3, 0)
-        for m in range(4):
-            half(m, 1)
-        move("g", hold[:, 0:16].bitcast(I32), w_codes[:, 1, HID - 16 : HID].bitcast(I32))
-        spread_four(1)
-        edge_prep(1, "ss")
-        move("g", hold[:, 16:32].bitcast(I32), t_codes[1][:, 1024 - 16 : 1024].bitcast(I32))
-        spread_four(2)
-        spread_four(3)
+        wait_g(0, w_codes[:, 1, HID - 16 : HID])
+        half(0, 1)
+        spread_tile(4)
+        half(1, 1)
+        spread_tile(5)
+        half(2, 1)
+        spread_tile(6)
+        half(3, 1)
+        spread_tile(7)
+        edge_prep(2, "s")
+        edge_prep(3, "s")
+        spread_src("g", 1)
         for m in range(4, 15):
             for h in range(2):
                 half(m, h)
+            if m < 12:
+                spread_tile(m + 4)
         half(15, 0)
         narrow(TILES - 1, 1024, 512)
         narrow(TILES - 1, 1536, 256)

from contextlib import ExitStack

import concourse.mybir as mybir
from concourse.masks import make_identity

F32 = mybir.dt.float32
BF16 = mybir.dt.bfloat16
I32 = mybir.dt.int32
U32 = mybir.dt.uint32
U8 = mybir.dt.uint8
FP8X4 = mybir.dt.float8_e4m3fn_x4

P = 128
ROWS = 2048
HID = 2048
D_IN = 1024
TILES = 16
SLOTS = 8
FLOPS = 2 * ROWS * D_IN * HID


def tile_edge_update_only_pa_kernel(tc, node_fts, edge_fts, Wt, out):
    nc = tc.nc
    node_flat = node_fts.flatten_outer_dims()
    edge_flat = edge_fts.flatten_outer_dims()
    out_flat = out.flatten_outer_dims()
    edge_view = edge_flat.rearrange("(b r s) c -> r b (s c)", b=2, s=8)
    wt_view = Wt.rearrange("(c q s) k -> q c (s k)", q=P, s=2)
    out_view = out_flat.rearrange("(b r s) h -> r b s h", b=2, s=8)

    with ExitStack() as ctx:
        const = ctx.enter_context(tc.tile_pool(name="const", bufs=1))
        stage = ctx.enter_context(tc.tile_pool(name="stage", bufs=4))
        ypool = ctx.enter_context(tc.tile_pool(name="ypool", bufs=4))
        opool = ctx.enter_context(tc.tile_pool(name="opool", bufs=8))
        psum = ctx.enter_context(tc.psum_pool(name="psum", bufs=8))
        ctx.enter_context(tc.manual_schedule())

        node_sb = const.tile([P, 1024], BF16)
        edge_sb = const.tile([P, 16 * 256], BF16)
        wt_sb = const.tile([P, 8, 2048], BF16)
        ident = const.tile([P, P], F32)
        warm_sb = const.tile([P, 512], BF16)
        small_in = const.tile([P, 1280], BF16, align_bytes=64)
        small_codes = const.tile([P, 320], U32, align_bytes=64)
        small_plane = const.tile([P, 320], U8, align_bytes=64)
        w_codes = const.tile([P, 2, HID], U32, align_bytes=64)
        w_plane = const.tile([P, 2, HID], U8, align_bytes=64)
        t_codes = [const.tile([P, (P * SLOTS, ROWS)[g]], U32, align_bytes=64, name="t_codes%d" % g) for g in range(2)]
        t_plane = [const.tile([P, (P * SLOTS, ROWS)[g]], U8, align_bytes=64, name="t_plane%d" % g) for g in range(2)]

        nc.vector.memset(warm_sb[:], 0.0)
        nc.vector.memset(node_sb[64:128, :], 0.0)
        nc.vector.memset(node_sb[0:64, 768:1024], 0.0)
        nc.vector.memset(t_plane[1][:, 0:1024].bitcast(I32), 0)
        nc.vector.memset(small_plane[:].bitcast(I32), 0)
        nc.gpsimd.memset(small_in[96:128, 0:1024].bitcast(F32), 0.0)
        def load_node():
            nc.sync.dma_start(out=node_sb[0:64, 0:384], in_=node_flat)
            nc.sync.dma_start(out=node_sb[0:64, 384:768], in_=node_flat)

        def load_edge(t0, t1):
            b, s0 = divmod(t0, 8)
            nc.sync.dma_start(
                out=edge_sb[:, 256 * t0 : 256 * t1], in_=edge_view[:, b, 256 * s0 : 256 * (s0 + t1 - t0)]
            )

        def load_w(c):
            nc.sync.dma_start(out=wt_sb[:, c, :], in_=wt_view[:, c, :])

        load_node()
        load_edge(0, 4)
        for c in range(6):
            load_w(c)
        make_identity(nc, ident[:])

        def warm(n):
            for i in range(n):
                wp = psum.tile([P, 512], F32, tag="bank")
                nc.tensor.matmul(out=wp[:], lhsT=warm_sb[:, 0:P], rhs=warm_sb[:], start=True, stop=True)

        def bank_copy(eng, dst, src):
            if eng == "v":
                nc.vector.tensor_copy(out=dst, in_=src)
            else:
                nc.scalar.copy(out=dst, in_=src)

        def node_prep():
            node32 = node_sb[:].bitcast(F32).rearrange("r (g w u) -> r g u w", g=2, w=P, u=2)
            pn = psum.tile([P, 512], F32, tag="bank")
            for g in range(2):
                for u in range(2):
                    nc.tensor.transpose(pn[:, (2 * g + u) * P : (2 * g + u + 1) * P], node32[:, g, u, :], ident[:])
            small32 = small_in[:].bitcast(F32)
            nc.scalar.copy(
                out=small32[0:96, 0:512].rearrange("p (c rep u) -> p c rep u", c=64, rep=4, u=2),
                in_=pn[0:96, 0:256]
                .rearrange("p (u c) -> p c u", u=2)[:, 0:64, :]
                .unsqueeze(2)
                .to_broadcast([96, 64, 4, 2]),
            )
            for g, lo, hi in ((0, 96, 128), (1, 0, 128)):
                dst_in = pn[lo:hi, 256 * g : 256 * (g + 1)].rearrange("p (u z b kq s) -> p z b s kq u", u=2, z=2, b=2, kq=4, s=8)
                dst_out = small32[lo:hi, 512 * g : 512 * g + 128].rearrange(
                    "p (b s kq u) -> p b s kq u", b=2, s=8, kq=4, u=2
                )
                for b in range(2):
                    nc.scalar.copy(out=dst_out[:, b, :, :, :], in_=dst_in[:, 0, b, :, :, :])
            for c0, c1 in ((0, 256), (256, 320)):
                nc.vector.quantize_mx(
                    out=small_codes[:, c0:c1].bitcast(FP8X4),
                    scales=small_plane[:, c0:c1],
                    in_=small_in[:, 4 * c0 : 4 * c1],
                )

        def move(eng, dst, src):
            if eng == "g":
                nc.gpsimd.tensor_copy(out=dst, in_=src)
            else:
                nc.vector.tensor_copy(out=dst, in_=src)

        def spread_dst(eng, g, lo, hi, tcol0, m0, nm, step):
            tcols = slice(tcol0, tcol0 + P * nm)
            at = m0 % step
            scols = slice(256 * g + 4 * (m0 - at), 256 * g + 4 * (m0 - at + step * nm))
            move(
                eng,
                t_codes[g][lo:hi, tcols].bitcast(I32).rearrange("p (m i x) -> p m i x", m=nm, i=32, x=4),
                small_codes[lo:hi, scols]
                .bitcast(I32)
                .rearrange("p (m z x) -> p m z x", z=step, x=4)[:, :, at, :]
                .unsqueeze(2)
                .to_broadcast([hi - lo, nm, 32, 4]),
            )
            move(
                eng,
                t_plane[g][lo:hi, tcols].bitcast(I32).rearrange("p (m w) -> p m w", m=nm),
                small_plane[lo:hi, scols]
                .bitcast(I32)
                .rearrange("p (m z) -> p m z", z=step)[:, :, at]
                .unsqueeze(2)
                .to_broadcast([hi - lo, nm, 32]),
            )

        def spread_src(eng, b):
            tcols = slice(4 * P * b, 4 * P * (b + 1))
            scols = slice(P * b, P * (b + 1))
            move(
                eng,
                t_codes[0][0:96, tcols].bitcast(I32).rearrange("p (m r) -> p m r", m=4),
                small_codes[0:96, scols].bitcast(I32).unsqueeze(1).to_broadcast([96, 4, 128]),
            )
            move(
                eng,
                t_plane[0][0:96, tcols].bitcast(I32).rearrange("p (m w) -> p m w", m=4),
                small_plane[0:96, scols].bitcast(I32).unsqueeze(1).to_broadcast([96, 4, 32]),
            )

        def col0(m):
            return P * (4 * (m // 8) + m % 4)

        def col1(m):
            return 1024 * (1 - m % 2) + P * (m // 2)

        def spread_pass0(eng, m0, nm):
            spread_dst(eng, 0, 96, 128, col0(m0), m0, nm, 1)

        def spread_tile(m):
            spread_pass1("g", m % 2, m // 2, m // 2 + 1)
            spread_pass0("g", m, 1)

        def spread_pass1(eng, par, j0, j1):
            spread_dst(eng, 1, 0, 64, col1(2 * j0 + par), 2 * j0 + par, j1 - j0, 2)

        edge32 = edge_sb[:].bitcast(F32).rearrange("r (x u) -> r u x", u=2)

        def edge_prep(q, eng):
            g1 = stage.tile([P, 1024], BF16, align_bytes=64, tag="g1")
            pe_bank = psum.tile([P, 512], F32, tag="bank")
            for jj in range(2):
                j = 2 * q + jj
                for u in range(2):
                    nc.tensor.transpose(
                        pe_bank[:, (2 * jj + u) * P : (2 * jj + u + 1) * P],
                        edge32[:, u, P * j : P * (j + 1)],
                        ident[:],
                    )
            bank_copy(
                eng,
                g1[:].bitcast(F32).rearrange("p (jj r u) -> p jj r u", jj=2, u=2),
                pe_bank[:].rearrange("p (jj u r) -> p jj r u", jj=2, u=2),
            )
            cols = slice(256 * q, 256 * (q + 1))
            up = slice(1024 + 256 * q, 1024 + 256 * (q + 1))
            nc.vector.quantize_mx(out=t_codes[1][:, cols].bitcast(FP8X4), scales=t_plane[1][:, cols], in_=g1[:])
            nc.sync.dma_start(out=t_codes[1][64:128, up].bitcast(I32), in_=t_codes[1][0:64, cols].bitcast(I32))
            nc.sync.dma_start(out=t_plane[1][64:128, up].bitcast(I32), in_=t_plane[1][0:64, cols].bitcast(I32))

        wt32 = wt_sb[:].bitcast(F32).rearrange("q c (s g w u) -> q c s g u w", s=2, g=2, w=P, u=2)
        gws = {}

        def w_turn(c, engs):
            half = c % 2
            for g in range(2):
                if half == 0:
                    gws[g] = stage.tile([P, 2048], BF16, align_bytes=64, tag="gw", name="gw")
                pw = psum.tile([P, 512], F32, tag="bank")
                for s in range(2):
                    for u in range(2):
                        nc.tensor.transpose(
                            pw[:, (2 * s + u) * P : (2 * s + u + 1) * P], wt32[:, c, s, g, u, :], ident[:]
                        )
                bank_copy(
                    engs[g],
                    gws[g][:].bitcast(F32)[:, 512 * half : 512 * (half + 1)].rearrange("p (q x) -> p q x", x=4),
                    pw[:].rearrange("p (x q) -> p q x", x=4),
                )

        def w_quant(cp):
            cols = slice(512 * cp, 512 * (cp + 1))
            for g in range(2):
                nc.vector.quantize_mx(
                    out=w_codes[:, g, cols].bitcast(FP8X4), scales=w_plane[:, g, cols], in_=gws[g][:]
                )

        def sums(m, c0, width):
            rows = (slice(col0(m), col0(m) + P), slice(col1(m), col1(m) + P))
            cols = slice(c0, c0 + width)
            acc = psum.tile([P, width], F32, tag="bank")
            for g in range(2):
                nc.tensor.matmul_mx(
                    out=acc[:],
                    lhsT=t_codes[g][:, rows[g]].bitcast(FP8X4),
                    lhsT_scale=t_plane[g][:, rows[g]],
                    rhs=w_codes[:, g, cols].bitcast(FP8X4),
                    rhs_scale=w_plane[:, g, cols],
                    start=(g == 0),
                    stop=(g == 1),
                )
            return acc

        outs = {}

        def bank(m, cp):
            whole = False
            width = 2048 if whole else 1024
            key = (m, 0) if whole else (m, cp // 2)
            if key not in outs:
                outs[key] = opool.tile([P, width], F32, tag="o", name="o")
            o = outs[key]
            at = 512 * cp % width
            acc = sums(m, 512 * cp, 512)
            y = ypool.tile([P, 512], F32, tag="y")
            nc.scalar.copy(out=y[:], in_=acc[:])
            nc.vector.scalar_tensor_tensor(
                out=o[:, at : at + 512],
                in0=acc[:],
                scalar=0.1,
                in1=y[:],
                op0=mybir.AluOpType.mult,
                op1=mybir.AluOpType.max,
            )

        def store_half(m, h):
            nc.sync.dma_start(out=out_view[:, m // 8, m % 8, 1024 * h : 1024 * (h + 1)], in_=outs[(m, h)][:])

        def narrow(m, c0, width):
            acc = sums(m, c0, width)
            y = ypool.tile([P, width], F32, tag="y")
            o = opool.tile([P, width], F32, tag="o")
            nc.scalar.copy(out=y[:], in_=acc[:])
            nc.vector.scalar_tensor_tensor(
                out=o[:], in0=acc[:], scalar=0.1, in1=y[:], op0=mybir.AluOpType.mult, op1=mybir.AluOpType.max
            )
            nc.sync.dma_start(out=out_view[:, m // 8, m % 8, c0 : c0 + width], in_=o[:])

        def unit(m, hh):
            bank(m, 2 * hh)
            bank(m, 2 * hh + 1)

        def spread_four(k):
            spread_pass0("g", 4 * k, 4 * k + 2)
            spread_pass1("g", 0, 2 * k, 2 * k + 2)
            spread_pass1("g", 1, 2 * k, 2 * k + 2)
            spread_pass0("g", 4 * k + 2, 4 * k + 4)

        hold = const.tile([P, 32], U32)

        def half(m, h):
            bank(m, 2 * h)
            bank(m, 2 * h + 1)
            store_half(m, h)

        def W(c, engs="ss"):
            w_turn(c, engs)
            if c % 2 == 1:
                w_quant(c // 2)

        def wait_g(n, src):
            move("g", hold[:, 16 * n : 16 * n + 16].bitcast(I32), src.bitcast(I32))

        warm(4)
        node_prep()
        spread_src("v", 0)
        spread_pass0("v", 0, 4)
        edge_prep(0, "s")
        load_w(6)
        load_w(7)
        load_edge(4, 8)
        load_edge(8, 12)
        load_edge(12, 16)
        W(0, "ss")
        W(1, "sv")
        W(2, "ss")
        W(3, "sv")
        spread_pass1("v", 0, 0, 2)
        W(4, "ss")
        spread_pass1("v", 1, 0, 2)
        W(5, "ss")
        half(0, 0)
        half(1, 0)
        W(6, "ss")
        W(7, "ss")
        edge_prep(1, "s")
        half(2, 0)
        half(3, 0)
        wait_g(0, w_codes[:, 1, HID - 16 : HID])
        half(0, 1)
        spread_tile(4)
        half(1, 1)
        spread_tile(5)
        half(2, 1)
        spread_tile(6)
        half(3, 1)
        spread_tile(7)
        edge_prep(2, "s")
        edge_prep(3, "s")
        spread_src("g", 1)
        for m in range(4, 15):
            for h in range(2):
                half(m, h)
            if m < 12:
                spread_tile(m + 4)
        half(15, 0)
        narrow(TILES - 1, 1024, 512)
        narrow(TILES - 1, 1536, 256)
        narrow(TILES - 1, 1792, 256)
